import numpy as np
import ml_dtypes


def mxq(x, axis, fmt="e4m3"):
    dtype, down = {"e4m3": (ml_dtypes.float8_e4m3fn, 7), "e5m2": (ml_dtypes.float8_e5m2, 14)}[fmt]
    v = np.moveaxis(np.asarray(x, np.float32).astype(ml_dtypes.bfloat16).astype(np.float64), axis, -1)
    blocks = v.reshape(v.shape[:-1] + (-1, 32))
    amax = np.abs(blocks).max(-1, keepdims=True)
    byte = np.maximum(np.where(amax > 0, np.frexp(amax)[1] - 1 + 127, 0) - down, 1)
    scale = np.exp2(byte - 127.0)
    codes = (blocks / scale).astype(np.float32).astype(dtype).astype(np.float64)
    return np.moveaxis((codes * scale).reshape(v.shape), -1, axis)


WIDE = False


def mx_kscale(k):
    if not WIDE:
        return np.ones(k)
    levels = np.array([10, -10, 5, -5, 0])
    if k % 512:
        return np.exp2(np.random.permutation(np.resize(levels, k // 32))).repeat(32)
    a = np.empty((k // 512, 16))
    for p in range(k // 512):
        a[p, :8] = np.random.permutation(np.resize(levels, 8))
        for g in range(8):
            far = levels[np.abs(levels - a[p, g]) >= 10]
            a[p, g + 8] = far[np.random.randint(len(far))]
    return np.exp2(a.ravel()).repeat(32)


BF16 = ml_dtypes.bfloat16


def bf(x):
    return np.asarray(x, np.float32).astype(BF16)


def f64(x):
    return np.asarray(x).astype(np.float64)


B, S, HID, H, KVH, D, QB = 1, 1024, 1024, 16, 4, 128, 512


def rope_tables():
    inv_freq = 1.0 / (10000.0 ** (np.arange(0, D, 2) / D))
    freqs = np.outer(np.arange(S), inv_freq)
    emb = np.concatenate([freqs, freqs], axis=-1)
    return np.cos(emb)[:, None, :], np.sin(emb)[:, None, :]


def rotate_half(x):
    x1, x2 = np.split(x, 2, axis=-1)
    return np.concatenate([-x2, x1], axis=-1)


def setup_inputs():
    s = mx_kscale(HID)
    cos, sin = rope_tables()
    return {"hidden_states": bf(np.random.standard_normal((B, S, HID)) * s),
            "cos": bf(cos),
            "sin": bf(sin),
            "wq": bf(np.random.standard_normal((H * D, HID)) * 1.5 / np.sqrt(HID) / s),
            "wk": bf(np.random.standard_normal((KVH * D, HID)) * 1.5 / np.sqrt(HID) / s),
            "wv": bf(np.random.standard_normal((KVH * D, HID)) / np.sqrt(HID) / s)}


def reference(hidden_states, cos, sin, wq, wk, wv):
    x = f64(hidden_states)
    b, n, _ = x.shape
    xq = mxq(x, 2, "e4m3")
    q = (xq @ mxq(f64(wq), 1, "e4m3").T).reshape(b, n, H, D)
    k = (xq @ mxq(f64(wk), 1, "e4m3").T).reshape(b, n, KVH, D)
    v = (xq @ mxq(f64(wv), 1, "e4m3").T).reshape(b, n, KVH, D)
    c, sn = f64(cos)[:n], f64(sin)[:n]
    q_rot = q * c + rotate_half(q) * sn
    k_rot = k * c + rotate_half(k) * sn
    return q_rot, k_rot, v

@@ -1,0 +1,162 @@
+from contextlib import ExitStack
+
+import concourse.mybir as mybir
+from concourse.masks import make_identity
+
+F32 = mybir.dt.float32
+BF16 = mybir.dt.bfloat16
+U32 = mybir.dt.uint32
+U8 = mybir.dt.uint8
+FP8X4 = mybir.dt.float8_e4m3fn_x4
+MULT = mybir.AluOpType.mult
+ADD = mybir.AluOpType.add
+
+P = 128
+K = 1024
+K_PASS = 512
+PASSES = K // K_PASS
+WORDS = K // 2
+TILES = 4
+CHUNK = TILES * P
+TOKEN_TILES = 8
+PAIRS = TOKEN_TILES // 2
+D = 128
+HALF = D // 2
+HEADS = CHUNK // D
+Q_CHUNKS = 4
+
+FLOPS = 2 * 1024 * 1024 * 3072
+
+
+def tile_attention_pa_kernel(tc, hidden_states, cos, sin, wq, wk, wv, out_0, out_1, out_2):
+    nc = tc.nc
+    with ExitStack() as ctx:
+        ctx.enter_context(tc.manual_schedule())
+        const = ctx.enter_context(tc.tile_pool(name="const", bufs=1))
+        raw_pool = ctx.enter_context(tc.tile_pool(name="raw", bufs=1))
+        mx_pool = ctx.enter_context(tc.tile_pool(name="mx", bufs=1))
+        grouped_pool = ctx.enter_context(tc.tile_pool(name="grouped", bufs=3))
+        prod_pool = ctx.enter_context(tc.tile_pool(name="prod", bufs=4))
+        rotated_pool = ctx.enter_context(tc.tile_pool(name="rotated", bufs=6))
+        plain_pool = ctx.enter_context(tc.tile_pool(name="plain", bufs=3))
+        scalar_banks = ctx.enter_context(tc.psum_pool(name="scalar_banks", bufs=4))
+        vector_banks = ctx.enter_context(tc.psum_pool(name="vector_banks", bufs=4))
+
+        x_rows = hidden_states[0].rearrange("(p t) k -> p t k", t=TOKEN_TILES)
+        q_out = out_0[0].rearrange("(p t) h d -> p t (h d)", t=TOKEN_TILES)
+        k_out = out_1[0].rearrange("(p t) h d -> p t (h d)", t=TOKEN_TILES)
+        v_out = out_2[0].rearrange("(p t) h d -> p t (h d)", t=TOKEN_TILES)
+
+        def weight_rows(w, c):
+            return w[c * CHUNK : (c + 1) * CHUNK, :].rearrange("(i r) k -> r i k", r=P)
+
+        rotated_rows = [weight_rows(wq, c) for c in range(Q_CHUNKS)] + [weight_rows(wk, 0)]
+        rotated_out = [q_out[:, :, c * CHUNK : (c + 1) * CHUNK] for c in range(Q_CHUNKS)] + [k_out]
+
+        def load(rows, name):
+            raw = raw_pool.tile([P, TILES * K], BF16, name=name)
+            for i in range(TILES):
+                nc.sync.dma_start(out=raw[:, i * K : (i + 1) * K], in_=rows[:, i, :])
+            return raw
+
+        x_raw = [load(x_rows[:, 0:TILES, :], "x_raw0")]
+        w_raw = [load(rotated_rows[0], "w_raw0")]
+        tables = const.tile([P, 2, TOKEN_TILES, D], BF16)
+        nc.sync.dma_start(out=tables[:, 0], in_=cos.rearrange("(p t) o d -> p t (o d)", t=TOKEN_TILES))
+        nc.sync.dma_start(out=tables[:, 1], in_=sin.rearrange("(p t) o d -> p t (o d)", t=TOKEN_TILES))
+        x_raw.append(load(x_rows[:, TILES : 2 * TILES, :], "x_raw1"))
+        w_raw.append(load(rotated_rows[1], "w_raw1"))
+        v_raw = load(weight_rows(wv, 0), "v_raw")
+        for n in range(2, len(rotated_rows)):
+            w_raw.append(load(rotated_rows[n], "w_raw%d" % n))
+
+        identity = const.tile([P, P], F32)
+        make_identity(nc, identity[:])
+
+        def prepare(raw, name):
+            words = raw[:].bitcast(F32)
+            grouped = grouped_pool.tile([P, PASSES * CHUNK * 4], BF16, align_bytes=64)
+            grouped_words = grouped[:].bitcast(F32).rearrange("p (g c u) -> p g c u", g=PASSES, u=2)
+            for i in range(TILES):
+                bank = scalar_banks.tile([P, WORDS], F32, tag="bank")
+                for gu in range(WORDS // P):
+                    nc.tensor.transpose(
+                        bank[:, gu * P : (gu + 1) * P],
+                        words[:, i * WORDS + (gu // 2) * 2 * P + gu % 2 : i * WORDS + (gu // 2 + 1) * 2 * P : 2],
+                        identity[:],
+                    )
+                nc.scalar.copy(
+                    out=grouped_words[:, :, i * P : (i + 1) * P, :],
+                    in_=bank[:].rearrange("p (g u r) -> p g r u", g=PASSES, u=2),
+                )
+            codes = mx_pool.tile([P, PASSES * CHUNK], U32, name=name + "_codes", align_bytes=64)
+            scales = mx_pool.tile([P, PASSES * CHUNK], U8, name=name + "_scales", align_bytes=64)
+            nc.vector.quantize_mx(out=codes[:].bitcast(FP8X4), scales=scales[:], in_=grouped[:])
+            return codes, scales
+
+        def project(bank, t, weights):
+            x_codes, x_scales = x_mx[t // TILES]
+            w_codes, w_scales = weights
+            for g in range(PASSES):
+                tokens = slice(g * CHUNK + (t % TILES) * P, g * CHUNK + (t % TILES + 1) * P)
+                features = slice(g * CHUNK, (g + 1) * CHUNK)
+                nc.tensor.matmul_mx(
+                    out=bank[:],
+                    lhsT=x_codes[:, tokens].bitcast(FP8X4),
+                    lhsT_scale=x_scales[:, tokens],
+                    rhs=w_codes[:, features].bitcast(FP8X4),
+                    rhs_scale=w_scales[:, features],
+                    start=(g == 0),
+                    stop=(g == PASSES - 1),
+                )
+
+        x_mx = [prepare(x_raw[0], "x0")]
+        w_mx = [prepare(w_raw[0], "w0")]
+        v_mx = []
+
+        rot = const.tile([P, TOKEN_TILES, 2, 2, HALF], BF16)
+        nc.vector.tensor_copy(out=rot[:, :, 0, 0, :], in_=tables[:, 0, :, 0:HALF])
+        nc.vector.tensor_copy(out=rot[:, :, 1, 1, :], in_=tables[:, 0, :, HALF:D])
+        nc.vector.tensor_copy(out=rot[:, :, 0, 1, :], in_=tables[:, 1, :, HALF:D])
+        nc.vector.tensor_scalar_mul(out=rot[:, :, 1, 0, :], in0=tables[:, 1, :, 0:HALF], scalar1=-1.0)
+
+        def rotated_pair(n, pair, adder):
+            prod = prod_pool.tile([P, 2 * HEADS, 2, D], F32)
+            for tt in range(2):
+                t = 2 * pair + tt
+                acc = vector_banks.tile([P, CHUNK], F32)
+                project(acc, t, w_mx[n])
+                nc.vector.tensor_tensor(
+                    out=prod[:, tt * HEADS : (tt + 1) * HEADS, :, :].rearrange("p h s (o j) -> p h s o j", o=2),
+                    in0=acc[:]
+                    .rearrange("p (h s j) -> p h s j", s=2, j=HALF)
+                    .unsqueeze(3)
+                    .to_broadcast([P, HEADS, 2, 2, HALF]),
+                    in1=rot[:, t].unsqueeze(1).to_broadcast([P, HEADS, 2, 2, HALF]),
+                    op=MULT,
+                )
+            rotated = rotated_pool.tile([P, 2 * HEADS, D], F32)
+            adder.tensor_tensor(out=rotated[:], in0=prod[:, :, 0, :], in1=prod[:, :, 1, :], op=ADD)
+            nc.sync.dma_start(
+                out=rotated_out[n][:, 2 * pair : 2 * pair + 2, :],
+                in_=rotated[:].rearrange("p (tt h) d -> p tt (h d)", tt=2),
+            )
+
+        def plain_pair(pair):
+            plain = plain_pool.tile([P, 2, CHUNK], F32)
+            for tt in range(2):
+                bank = scalar_banks.tile([P, CHUNK], F32, tag="bank")
+                project(bank, 2 * pair + tt, v_mx[0])
+                nc.scalar.copy(out=plain[:, tt, :], in_=bank[:])
+            nc.sync.dma_start(out=v_out[:, 2 * pair : 2 * pair + 2, :], in_=plain[:])
+
+        waiting = [(x_raw[1], x_mx, "x1"), (w_raw[1], w_mx, "w1"), (v_raw, v_mx, "v")]
+        waiting += [(w_raw[n], w_mx, "w%d" % n) for n in range(2, len(w_raw))]
+        rotated_pairs = len(w_raw) * PAIRS
+        for step in range(rotated_pairs):
+            rotated_pair(step // PAIRS, step % PAIRS, nc.vector if step == rotated_pairs - 1 else nc.gpsimd)
+            if step < len(waiting):
+                raw, prepared, name = waiting[step]
+                prepared.append(prepare(raw, name))
+            elif step < len(waiting) + PAIRS:
+                plain_pair(step - len(waiting))

@@ -19,7 +19,6 @@ WORDS = K // 2
 TILES = 4
 CHUNK = TILES * P
 TOKEN_TILES = 8
-PAIRS = TOKEN_TILES // 2
 D = 128
 HALF = D // 2
 HEADS = CHUNK // D
@@ -35,7 +34,9 @@ def tile_attention_pa_kernel(tc, hidden_states, cos, sin, wq, wk, wv, out_0, out
         const = ctx.enter_context(tc.tile_pool(name="const", bufs=1))
         raw_pool = ctx.enter_context(tc.tile_pool(name="raw", bufs=1))
         mx_pool = ctx.enter_context(tc.tile_pool(name="mx", bufs=1))
-        grouped_pool = ctx.enter_context(tc.tile_pool(name="grouped", bufs=3))
+        tile_grouped_pool = ctx.enter_context(tc.tile_pool(name="tile_grouped", bufs=4))
+        half_grouped_pool = ctx.enter_context(tc.tile_pool(name="half_grouped", bufs=2))
+        w_grouped_pool = ctx.enter_context(tc.tile_pool(name="w_grouped", bufs=2))
         prod_pool = ctx.enter_context(tc.tile_pool(name="prod", bufs=4))
         rotated_pool = ctx.enter_context(tc.tile_pool(name="rotated", bufs=6))
         plain_pool = ctx.enter_context(tc.tile_pool(name="plain", bufs=3))
@@ -54,17 +55,24 @@ def tile_attention_pa_kernel(tc, hidden_states, cos, sin, wq, wk, wv, out_0, out
         rotated_out = [q_out[:, :, c * CHUNK : (c + 1) * CHUNK] for c in range(Q_CHUNKS)] + [k_out]
 
         def load(rows, name):
-            raw = raw_pool.tile([P, TILES * K], BF16, name=name)
+            raw = raw_pool.tile([P, TILES, K], BF16, name=name)
             for i in range(TILES):
-                nc.sync.dma_start(out=raw[:, i * K : (i + 1) * K], in_=rows[:, i, :])
+                nc.sync.dma_start(out=raw[:, i, :], in_=rows[:, i, :])
             return raw
 
-        x_raw = [load(x_rows[:, 0:TILES, :], "x_raw0")]
+        x_raw = raw_pool.tile([P, TOKEN_TILES, K], BF16)
+
+        def load_x(t):
+            nc.sync.dma_start(out=x_raw[:, t, :], in_=x_rows[:, t, :])
+
+        load_x(0)
         w_raw = [load(rotated_rows[0], "w_raw0")]
+        load_x(1)
         tables = const.tile([P, 2, TOKEN_TILES, D], BF16)
         nc.sync.dma_start(out=tables[:, 0], in_=cos.rearrange("(p t) o d -> p t (o d)", t=TOKEN_TILES))
         nc.sync.dma_start(out=tables[:, 1], in_=sin.rearrange("(p t) o d -> p t (o d)", t=TOKEN_TILES))
-        x_raw.append(load(x_rows[:, TILES : 2 * TILES, :], "x_raw1"))
+        for t in range(2, TOKEN_TILES):
+            load_x(t)
         w_raw.append(load(rotated_rows[1], "w_raw1"))
         v_raw = load(weight_rows(wv, 0), "v_raw")
         for n in range(2, len(rotated_rows)):
@@ -73,90 +81,158 @@ def tile_attention_pa_kernel(tc, hidden_states, cos, sin, wq, wk, wv, out_0, out
         identity = const.tile([P, P], F32)
         make_identity(nc, identity[:])
 
-        def prepare(raw, name):
-            words = raw[:].bitcast(F32)
-            grouped = grouped_pool.tile([P, PASSES * CHUNK * 4], BF16, align_bytes=64)
-            grouped_words = grouped[:].bitcast(F32).rearrange("p (g c u) -> p g c u", g=PASSES, u=2)
-            for i in range(TILES):
-                bank = scalar_banks.tile([P, WORDS], F32, tag="bank")
-                for gu in range(WORDS // P):
+        def transpose_tile(rows, grouped):
+            words = rows.bitcast(F32)
+            bank = scalar_banks.tile([P, WORDS], F32, tag="bank")
+            for g in range(PASSES):
+                for u in range(2):
                     nc.tensor.transpose(
-                        bank[:, gu * P : (gu + 1) * P],
-                        words[:, i * WORDS + (gu // 2) * 2 * P + gu % 2 : i * WORDS + (gu // 2 + 1) * 2 * P : 2],
+                        bank[:, (2 * g + u) * P : (2 * g + u + 1) * P],
+                        words[:, 2 * g * P + u : 2 * (g + 1) * P : 2],
                         identity[:],
                     )
-                nc.scalar.copy(
-                    out=grouped_words[:, :, i * P : (i + 1) * P, :],
-                    in_=bank[:].rearrange("p (g u r) -> p g r u", g=PASSES, u=2),
-                )
+            nc.scalar.copy(out=grouped, in_=bank[:].rearrange("p (g u r) -> p g r u", g=PASSES, u=2))
+
+        x_codes = mx_pool.tile([P, TOKEN_TILES, PASSES * P], U32, align_bytes=64)
+        x_scales = mx_pool.tile([P, TOKEN_TILES, PASSES * P], U8, align_bytes=64)
+
+        def transpose_x(t):
+            grouped = tile_grouped_pool.tile([P, PASSES * P * 4], BF16, align_bytes=64)
+            transpose_tile(x_raw[:, t, :], grouped[:].bitcast(F32).rearrange("p (g r u) -> p g r u", g=PASSES, u=2))
+            return grouped
+
+        def quantise_x(t, grouped):
+            nc.vector.quantize_mx(out=x_codes[:, t, :].bitcast(FP8X4), scales=x_scales[:, t, :], in_=grouped[:])
+
+        def mx_tiles(name):
             codes = mx_pool.tile([P, PASSES * CHUNK], U32, name=name + "_codes", align_bytes=64)
             scales = mx_pool.tile([P, PASSES * CHUNK], U8, name=name + "_scales", align_bytes=64)
-            nc.vector.quantize_mx(out=codes[:].bitcast(FP8X4), scales=scales[:], in_=grouped[:])
             return codes, scales
 
+        def transpose_w(raw, tiles, pool):
+            columns = len(tiles) * P
+            grouped = pool.tile([P, PASSES * columns * 4], BF16, align_bytes=64)
+            view = grouped[:].bitcast(F32).rearrange("p (g c u) -> p g c u", g=PASSES, u=2)
+            for i, tile in enumerate(tiles):
+                transpose_tile(raw[:, tile, :], view[:, :, i * P : (i + 1) * P, :])
+            return grouped
+
+        def quantise_w(weights, tiles, grouped):
+            codes, scales = weights
+            columns = len(tiles) * P
+            runs = 1 if columns == CHUNK else PASSES
+            width = PASSES * columns // runs
+            for g in range(runs):
+                first = g * CHUNK + tiles[0] * P
+                nc.vector.quantize_mx(
+                    out=codes[:, first : first + width].bitcast(FP8X4),
+                    scales=scales[:, first : first + width],
+                    in_=grouped[:, 4 * g * width : 4 * (g + 1) * width],
+                )
+
         def project(bank, t, weights):
-            x_codes, x_scales = x_mx[t // TILES]
             w_codes, w_scales = weights
             for g in range(PASSES):
-                tokens = slice(g * CHUNK + (t % TILES) * P, g * CHUNK + (t % TILES + 1) * P)
+                tokens = slice(g * P, (g + 1) * P)
                 features = slice(g * CHUNK, (g + 1) * CHUNK)
                 nc.tensor.matmul_mx(
                     out=bank[:],
-                    lhsT=x_codes[:, tokens].bitcast(FP8X4),
-                    lhsT_scale=x_scales[:, tokens],
+                    lhsT=x_codes[:, t, tokens].bitcast(FP8X4),
+                    lhsT_scale=x_scales[:, t, tokens],
                     rhs=w_codes[:, features].bitcast(FP8X4),
                     rhs_scale=w_scales[:, features],
                     start=(g == 0),
                     stop=(g == PASSES - 1),
                 )
 
-        x_mx = [prepare(x_raw[0], "x0")]
-        w_mx = [prepare(w_raw[0], "w0")]
-        v_mx = []
-
         rot = const.tile([P, TOKEN_TILES, 2, 2, HALF], BF16)
-        nc.vector.tensor_copy(out=rot[:, :, 0, 0, :], in_=tables[:, 0, :, 0:HALF])
-        nc.vector.tensor_copy(out=rot[:, :, 1, 1, :], in_=tables[:, 0, :, HALF:D])
-        nc.vector.tensor_copy(out=rot[:, :, 0, 1, :], in_=tables[:, 1, :, HALF:D])
-        nc.vector.tensor_scalar_mul(out=rot[:, :, 1, 0, :], in0=tables[:, 1, :, 0:HALF], scalar1=-1.0)
 
-        def rotated_pair(n, pair, adder):
-            prod = prod_pool.tile([P, 2 * HEADS, 2, D], F32)
-            for tt in range(2):
-                t = 2 * pair + tt
-                acc = vector_banks.tile([P, CHUNK], F32)
-                project(acc, t, w_mx[n])
-                nc.vector.tensor_tensor(
-                    out=prod[:, tt * HEADS : (tt + 1) * HEADS, :, :].rearrange("p h s (o j) -> p h s o j", o=2),
-                    in0=acc[:]
-                    .rearrange("p (h s j) -> p h s j", s=2, j=HALF)
-                    .unsqueeze(3)
-                    .to_broadcast([P, HEADS, 2, 2, HALF]),
-                    in1=rot[:, t].unsqueeze(1).to_broadcast([P, HEADS, 2, 2, HALF]),
-                    op=MULT,
-                )
-            rotated = rotated_pool.tile([P, 2 * HEADS, D], F32)
-            adder.tensor_tensor(out=rotated[:], in0=prod[:, :, 0, :], in1=prod[:, :, 1, :], op=ADD)
-            nc.sync.dma_start(
-                out=rotated_out[n][:, 2 * pair : 2 * pair + 2, :],
-                in_=rotated[:].rearrange("p (tt h) d -> p tt (h d)", tt=2),
+        def build_rotation():
+            nc.vector.tensor_copy(out=rot[:, :, 0, 0, :], in_=tables[:, 0, :, 0:HALF])
+            nc.vector.tensor_copy(out=rot[:, :, 1, 1, :], in_=tables[:, 0, :, HALF:D])
+            nc.vector.tensor_copy(out=rot[:, :, 0, 1, :], in_=tables[:, 1, :, HALF:D])
+            nc.vector.tensor_scalar_mul(out=rot[:, :, 1, 0, :], in0=tables[:, 1, :, 0:HALF], scalar1=-1.0)
+
+        def products(prod, t, n):
+            acc = vector_banks.tile([P, CHUNK], F32)
+            project(acc, t, w_mx[n])
+            nc.vector.tensor_tensor(
+                out=prod.rearrange("p h s (o j) -> p h s o j", o=2),
+                in0=acc[:]
+                .rearrange("p (h s j) -> p h s j", s=2, j=HALF)
+                .unsqueeze(3)
+                .to_broadcast([P, HEADS, 2, 2, HALF]),
+                in1=rot[:, t].unsqueeze(1).to_broadcast([P, HEADS, 2, 2, HALF]),
+                op=MULT,
             )
 
-        def plain_pair(pair):
-            plain = plain_pool.tile([P, 2, CHUNK], F32)
-            for tt in range(2):
-                bank = scalar_banks.tile([P, CHUNK], F32, tag="bank")
-                project(bank, 2 * pair + tt, v_mx[0])
-                nc.scalar.copy(out=plain[:, tt, :], in_=bank[:])
-            nc.sync.dma_start(out=v_out[:, 2 * pair : 2 * pair + 2, :], in_=plain[:])
+        def add(rotated, prod, adder):
+            adder.tensor_tensor(out=rotated, in0=prod[:, :, 0, :], in1=prod[:, :, 1, :], op=ADD)
 
-        waiting = [(x_raw[1], x_mx, "x1"), (w_raw[1], w_mx, "w1"), (v_raw, v_mx, "v")]
-        waiting += [(w_raw[n], w_mx, "w%d" % n) for n in range(2, len(w_raw))]
-        rotated_pairs = len(w_raw) * PAIRS
-        for step in range(rotated_pairs):
-            rotated_pair(step // PAIRS, step % PAIRS, nc.vector if step == rotated_pairs - 1 else nc.gpsimd)
-            if step < len(waiting):
-                raw, prepared, name = waiting[step]
-                prepared.append(prepare(raw, name))
-            elif step < len(waiting) + PAIRS:
-                plain_pair(step - len(waiting))
+        def store(rotated, n, first, last):
+            nc.sync.dma_start(
+                out=rotated_out[n][:, first:last, :],
+                in_=rotated.rearrange("p (t h) d -> p t (h d)", h=HEADS),
+            )
+
+        grouped = transpose_x(0)
+        quantise_x(0, grouped)
+        w_mx = [mx_tiles("w%d" % n) for n in range(len(w_raw))]
+        v_mx = mx_tiles("v")
+        for i in range(TILES):
+            grouped = transpose_w(w_raw[0], [i], tile_grouped_pool)
+            quantise_w(w_mx[0], [i], grouped)
+        grouped = transpose_x(1)
+        quantise_x(1, grouped)
+        build_rotation()
+
+        plain_tiles = []
+
+        def plain_tile(t):
+            if t % 2 == 0:
+                plain = plain_pool.tile([P, 2, CHUNK], F32)
+                plain_tiles.append(plain)
+            plain = plain_tiles[-1]
+            bank = scalar_banks.tile([P, CHUNK], F32, tag="bank")
+            project(bank, t, v_mx)
+            nc.scalar.copy(out=plain[:, t % 2, :], in_=bank[:])
+            if t % 2 == 1:
+                nc.sync.dma_start(out=v_out[:, t - 1 : t + 1, :], in_=plain[:])
+
+        all_tiles = list(range(TILES))
+        last_chunk = len(w_raw) - 1
+        for n in range(len(w_raw)):
+            for t in range(TOKEN_TILES):
+                if t % 2 == 0:
+                    rotated = rotated_pool.tile([P, 2 * HEADS, D], F32)
+                    prod = prod_pool.tile([P, 2 * HEADS, 2, D], F32)
+                heads = slice((t % 2) * HEADS, (t % 2 + 1) * HEADS)
+                products(prod[:, heads], t, n)
+                if n == last_chunk and t >= TOKEN_TILES - 2:
+                    add(rotated[:, heads], prod[:, heads], nc.vector if t == TOKEN_TILES - 1 else nc.gpsimd)
+                    store(rotated[:, heads], n, t, t + 1)
+                elif t % 2 == 1:
+                    add(rotated[:], prod[:], nc.gpsimd)
+                    store(rotated[:], n, t - 1, t + 1)
+                if n == 0:
+                    if t + 2 < TOKEN_TILES:
+                        x_grouped = transpose_x(t + 2)
+                    if t in (4, 6):
+                        grouped = transpose_w(w_raw[1], [t - 4, t - 3], half_grouped_pool)
+                    if t + 2 < TOKEN_TILES:
+                        quantise_x(t + 2, x_grouped)
+                    if t in (5, 6):
+                        first = 2 * (t - 5)
+                        quantise_w(w_mx[1], [first, first + 1], grouped)
+                else:
+                    if n < last_chunk and t == 1:
+                        w_grouped = transpose_w(w_raw[n + 1], all_tiles, w_grouped_pool)
+                    if n < last_chunk and t == 4:
+                        quantise_w(w_mx[n + 1], all_tiles, w_grouped)
+                    if n == 1 and t == 5:
+                        v_grouped = transpose_w(v_raw, all_tiles, w_grouped_pool)
+                    if n == 2 and t == 0:
+                        quantise_w(v_mx, all_tiles, v_grouped)
+                    slot = (n - 2) * TOKEN_TILES + t
+                    if slot >= 2 and slot % 2 == 0 and slot // 2 <= TOKEN_TILES:
+                        plain_tile(slot // 2 - 1)

@@ -35,7 +35,6 @@ def tile_attention_pa_kernel(tc, hidden_states, cos, sin, wq, wk, wv, out_0, out
         raw_pool = ctx.enter_context(tc.tile_pool(name="raw", bufs=1))
         mx_pool = ctx.enter_context(tc.tile_pool(name="mx", bufs=1))
         tile_grouped_pool = ctx.enter_context(tc.tile_pool(name="tile_grouped", bufs=4))
-        half_grouped_pool = ctx.enter_context(tc.tile_pool(name="half_grouped", bufs=2))
         w_grouped_pool = ctx.enter_context(tc.tile_pool(name="w_grouped", bufs=2))
         prod_pool = ctx.enter_context(tc.tile_pool(name="prod", bufs=4))
         rotated_pool = ctx.enter_context(tc.tile_pool(name="rotated", bufs=6))
@@ -93,16 +92,19 @@ def tile_attention_pa_kernel(tc, hidden_states, cos, sin, wq, wk, wv, out_0, out
                     )
             nc.scalar.copy(out=grouped, in_=bank[:].rearrange("p (g u r) -> p g r u", g=PASSES, u=2))
 
-        x_codes = mx_pool.tile([P, TOKEN_TILES, PASSES * P], U32, align_bytes=64)
-        x_scales = mx_pool.tile([P, TOKEN_TILES, PASSES * P], U8, align_bytes=64)
+        x_codes = mx_pool.tile([P, TOKEN_TILES * PASSES * P], U32, align_bytes=64)
+        x_scales = mx_pool.tile([P, TOKEN_TILES * PASSES * P], U8, align_bytes=64)
 
-        def transpose_x(t):
-            grouped = tile_grouped_pool.tile([P, PASSES * P * 4], BF16, align_bytes=64)
-            transpose_tile(x_raw[:, t, :], grouped[:].bitcast(F32).rearrange("p (g r u) -> p g r u", g=PASSES, u=2))
+        def transpose_x(tiles):
+            grouped = tile_grouped_pool.tile([P, len(tiles) * PASSES * P * 4], BF16, align_bytes=64)
+            view = grouped[:].bitcast(F32).rearrange("p (t g r u) -> p t g r u", t=len(tiles), g=PASSES, u=2)
+            for i, t in enumerate(tiles):
+                transpose_tile(x_raw[:, t, :], view[:, i])
             return grouped
 
-        def quantise_x(t, grouped):
-            nc.vector.quantize_mx(out=x_codes[:, t, :].bitcast(FP8X4), scales=x_scales[:, t, :], in_=grouped[:])
+        def quantise_x(tiles, grouped):
+            span = slice(tiles[0] * PASSES * P, (tiles[-1] + 1) * PASSES * P)
+            nc.vector.quantize_mx(out=x_codes[:, span].bitcast(FP8X4), scales=x_scales[:, span], in_=grouped[:])
 
         def mx_tiles(name):
             codes = mx_pool.tile([P, PASSES * CHUNK], U32, name=name + "_codes", align_bytes=64)
@@ -133,12 +135,12 @@ def tile_attention_pa_kernel(tc, hidden_states, cos, sin, wq, wk, wv, out_0, out
         def project(bank, t, weights):
             w_codes, w_scales = weights
             for g in range(PASSES):
-                tokens = slice(g * P, (g + 1) * P)
+                tokens = slice((t * PASSES + g) * P, (t * PASSES + g + 1) * P)
                 features = slice(g * CHUNK, (g + 1) * CHUNK)
                 nc.tensor.matmul_mx(
                     out=bank[:],
-                    lhsT=x_codes[:, t, tokens].bitcast(FP8X4),
-                    lhsT_scale=x_scales[:, t, tokens],
+                    lhsT=x_codes[:, tokens].bitcast(FP8X4),
+                    lhsT_scale=x_scales[:, tokens],
                     rhs=w_codes[:, features].bitcast(FP8X4),
                     rhs_scale=w_scales[:, features],
                     start=(g == 0),
@@ -175,15 +177,15 @@ def tile_attention_pa_kernel(tc, hidden_states, cos, sin, wq, wk, wv, out_0, out
                 in_=rotated.rearrange("p (t h) d -> p t (h d)", h=HEADS),
             )
 
-        grouped = transpose_x(0)
-        quantise_x(0, grouped)
+        grouped = transpose_x([0])
+        quantise_x([0], grouped)
         w_mx = [mx_tiles("w%d" % n) for n in range(len(w_raw))]
         v_mx = mx_tiles("v")
         for i in range(TILES):
             grouped = transpose_w(w_raw[0], [i], tile_grouped_pool)
             quantise_w(w_mx[0], [i], grouped)
-        grouped = transpose_x(1)
-        quantise_x(1, grouped)
+        grouped = transpose_x([1])
+        quantise_x([1], grouped)
         build_rotation()
 
         plain_tiles = []
@@ -215,23 +217,29 @@ def tile_attention_pa_kernel(tc, hidden_states, cos, sin, wq, wk, wv, out_0, out
                     add(rotated[:], prod[:], nc.gpsimd)
                     store(rotated[:], n, t - 1, t + 1)
                 if n == 0:
-                    if t + 2 < TOKEN_TILES:
-                        x_grouped = transpose_x(t + 2)
-                    if t in (4, 6):
-                        grouped = transpose_w(w_raw[1], [t - 4, t - 3], half_grouped_pool)
-                    if t + 2 < TOKEN_TILES:
-                        quantise_x(t + 2, x_grouped)
-                    if t in (5, 6):
-                        first = 2 * (t - 5)
-                        quantise_w(w_mx[1], [first, first + 1], grouped)
+                    if t == 0:
+                        x_grouped = transpose_x([2])
+                        quantise_x([2], x_grouped)
+                    if t == 1:
+                        x_grouped = transpose_x([3])
+                        quantise_x([3], x_grouped)
+                        x_grouped = transpose_x([4, 5])
+                        quantise_x([4, 5], x_grouped)
+                    if t == 2:
+                        x_grouped = transpose_x([6, 7])
+                    if t == 3:
+                        quantise_x([6, 7], x_grouped)
+                        w_grouped = transpose_w(w_raw[1], all_tiles, w_grouped_pool)
+                    if t == 5:
+                        quantise_w(w_mx[1], all_tiles, w_grouped)
                 else:
                     if n < last_chunk and t == 1:
                         w_grouped = transpose_w(w_raw[n + 1], all_tiles, w_grouped_pool)
-                    if n < last_chunk and t == 4:
+                    if n < last_chunk and t == 5:
                         quantise_w(w_mx[n + 1], all_tiles, w_grouped)
                     if n == 1 and t == 5:
                         v_grouped = transpose_w(v_raw, all_tiles, w_grouped_pool)
-                    if n == 2 and t == 0:
+                    if n == 2 and t == 1:
                         quantise_w(v_mx, all_tiles, v_grouped)
                     slot = (n - 2) * TOKEN_TILES + t
                     if slot >= 2 and slot % 2 == 0 and slot // 2 <= TOKEN_TILES:

@@ -35,7 +35,7 @@ def tile_attention_pa_kernel(tc, hidden_states, cos, sin, wq, wk, wv, out_0, out
         raw_pool = ctx.enter_context(tc.tile_pool(name="raw", bufs=1))
         mx_pool = ctx.enter_context(tc.tile_pool(name="mx", bufs=1))
         tile_grouped_pool = ctx.enter_context(tc.tile_pool(name="tile_grouped", bufs=4))
-        w_grouped_pool = ctx.enter_context(tc.tile_pool(name="w_grouped", bufs=2))
+        w_grouped_pool = ctx.enter_context(tc.tile_pool(name="w_grouped", bufs=3))
         prod_pool = ctx.enter_context(tc.tile_pool(name="prod", bufs=4))
         rotated_pool = ctx.enter_context(tc.tile_pool(name="rotated", bufs=6))
         plain_pool = ctx.enter_context(tc.tile_pool(name="plain", bufs=3))
@@ -73,9 +73,9 @@ def tile_attention_pa_kernel(tc, hidden_states, cos, sin, wq, wk, wv, out_0, out
         for t in range(2, TOKEN_TILES):
             load_x(t)
         w_raw.append(load(rotated_rows[1], "w_raw1"))
-        v_raw = load(weight_rows(wv, 0), "v_raw")
         for n in range(2, len(rotated_rows)):
             w_raw.append(load(rotated_rows[n], "w_raw%d" % n))
+        v_raw = load(weight_rows(wv, 0), "v_raw")
 
         identity = const.tile([P, P], F32)
         make_identity(nc, identity[:])
@@ -209,13 +209,12 @@ def tile_attention_pa_kernel(tc, hidden_states, cos, sin, wq, wk, wv, out_0, out
                     rotated = rotated_pool.tile([P, 2 * HEADS, D], F32)
                     prod = prod_pool.tile([P, 2 * HEADS, 2, D], F32)
                 heads = slice((t % 2) * HEADS, (t % 2 + 1) * HEADS)
+                if n == 0 and t == 3:
+                    quantise_x([4, 5, 6, 7], x_grouped)
+                if n == 0 and t == 5:
+                    quantise_w(w_mx[1], all_tiles, w_grouped)
+                    quantise_w(w_mx[2], all_tiles, w_grouped_2)
                 products(prod[:, heads], t, n)
-                if n == last_chunk and t >= TOKEN_TILES - 2:
-                    add(rotated[:, heads], prod[:, heads], nc.vector if t == TOKEN_TILES - 1 else nc.gpsimd)
-                    store(rotated[:, heads], n, t, t + 1)
-                elif t % 2 == 1:
-                    add(rotated[:], prod[:], nc.gpsimd)
-                    store(rotated[:], n, t - 1, t + 1)
                 if n == 0:
                     if t == 0:
                         x_grouped = transpose_x([2])
@@ -223,24 +222,30 @@ def tile_attention_pa_kernel(tc, hidden_states, cos, sin, wq, wk, wv, out_0, out
                     if t == 1:
                         x_grouped = transpose_x([3])
                         quantise_x([3], x_grouped)
-                        x_grouped = transpose_x([4, 5])
-                        quantise_x([4, 5], x_grouped)
+                        x_grouped = transpose_x([4, 5, 6, 7])
                     if t == 2:
-                        x_grouped = transpose_x([6, 7])
-                    if t == 3:
-                        quantise_x([6, 7], x_grouped)
                         w_grouped = transpose_w(w_raw[1], all_tiles, w_grouped_pool)
-                    if t == 5:
-                        quantise_w(w_mx[1], all_tiles, w_grouped)
-                else:
-                    if n < last_chunk and t == 1:
-                        w_grouped = transpose_w(w_raw[n + 1], all_tiles, w_grouped_pool)
-                    if n < last_chunk and t == 5:
-                        quantise_w(w_mx[n + 1], all_tiles, w_grouped)
+                    if t == 4:
+                        w_grouped_2 = transpose_w(w_raw[2], all_tiles, w_grouped_pool)
+                if n == last_chunk and t >= TOKEN_TILES - 2:
+                    add(rotated[:, heads], prod[:, heads], nc.vector if t == TOKEN_TILES - 1 else nc.gpsimd)
+                    store(rotated[:, heads], n, t, t + 1)
+                elif t % 2 == 1:
+                    add(rotated[:], prod[:], nc.vector if n == 0 and t <= 3 else nc.gpsimd)
+                    store(rotated[:], n, t - 1, t + 1)
+                if n > 0:
+                    if n == 1 and t == 1:
+                        w_grouped = transpose_w(w_raw[3], all_tiles, w_grouped_pool)
+                    if n == 1 and t == 3:
+                        quantise_w(w_mx[3], all_tiles, w_grouped)
                     if n == 1 and t == 5:
-                        v_grouped = transpose_w(v_raw, all_tiles, w_grouped_pool)
+                        w_grouped = transpose_w(w_raw[4], all_tiles, w_grouped_pool)
+                    if n == 1 and t == 7:
+                        quantise_w(w_mx[4], all_tiles, w_grouped)
                     if n == 2 and t == 1:
-                        quantise_w(v_mx, all_tiles, v_grouped)
+                        w_grouped = transpose_w(v_raw, all_tiles, w_grouped_pool)
+                    if n == 2 and t == 3:
+                        quantise_w(v_mx, all_tiles, w_grouped)
                     slot = (n - 2) * TOKEN_TILES + t
-                    if slot >= 2 and slot % 2 == 0 and slot // 2 <= TOKEN_TILES:
-                        plain_tile(slot // 2 - 1)
+                    if slot >= 6 and slot % 2 == 0 and slot // 2 <= TOKEN_TILES + 2:
+                        plain_tile(slot // 2 - 3)

@@ -19,6 +19,7 @@ WORDS = K // 2
 TILES = 4
 CHUNK = TILES * P
 TOKEN_TILES = 8
+PAIRS = TOKEN_TILES // 2
 D = 128
 HALF = D // 2
 HEADS = CHUNK // D
@@ -35,9 +36,11 @@ def tile_attention_pa_kernel(tc, hidden_states, cos, sin, wq, wk, wv, out_0, out
         raw_pool = ctx.enter_context(tc.tile_pool(name="raw", bufs=1))
         mx_pool = ctx.enter_context(tc.tile_pool(name="mx", bufs=1))
         tile_grouped_pool = ctx.enter_context(tc.tile_pool(name="tile_grouped", bufs=4))
-        w_grouped_pool = ctx.enter_context(tc.tile_pool(name="w_grouped", bufs=3))
+        head_prod_pool = ctx.enter_context(tc.tile_pool(name="head_prod", bufs=4))
+        block_pool = ctx.enter_context(tc.tile_pool(name="block", bufs=2))
+        w_grouped_pool = ctx.enter_context(tc.tile_pool(name="w_grouped", bufs=2))
         prod_pool = ctx.enter_context(tc.tile_pool(name="prod", bufs=4))
-        rotated_pool = ctx.enter_context(tc.tile_pool(name="rotated", bufs=6))
+        rotated_pool = ctx.enter_context(tc.tile_pool(name="rotated", bufs=5))
         plain_pool = ctx.enter_context(tc.tile_pool(name="plain", bufs=3))
         scalar_banks = ctx.enter_context(tc.psum_pool(name="scalar_banks", bufs=4))
         vector_banks = ctx.enter_context(tc.psum_pool(name="vector_banks", bufs=4))
@@ -59,10 +62,10 @@ def tile_attention_pa_kernel(tc, hidden_states, cos, sin, wq, wk, wv, out_0, out
                 nc.sync.dma_start(out=raw[:, i, :], in_=rows[:, i, :])
             return raw
 
-        x_raw = raw_pool.tile([P, TOKEN_TILES, K], BF16)
+        x_raw = [raw_pool.tile([P, TILES, K], BF16, name="x_raw%d" % h) for h in range(2)]
 
         def load_x(t):
-            nc.sync.dma_start(out=x_raw[:, t, :], in_=x_rows[:, t, :])
+            nc.sync.dma_start(out=x_raw[t // TILES][:, t % TILES, :], in_=x_rows[:, t, :])
 
         load_x(0)
         w_raw = [load(rotated_rows[0], "w_raw0")]
@@ -72,13 +75,18 @@ def tile_attention_pa_kernel(tc, hidden_states, cos, sin, wq, wk, wv, out_0, out
         nc.sync.dma_start(out=tables[:, 1], in_=sin.rearrange("(p t) o d -> p t (o d)", t=TOKEN_TILES))
         for t in range(2, TOKEN_TILES):
             load_x(t)
-        w_raw.append(load(rotated_rows[1], "w_raw1"))
-        for n in range(2, len(rotated_rows)):
+        for n in range(1, Q_CHUNKS):
             w_raw.append(load(rotated_rows[n], "w_raw%d" % n))
         v_raw = load(weight_rows(wv, 0), "v_raw")
+        w_raw.append(load(rotated_rows[Q_CHUNKS], "w_raw%d" % Q_CHUNKS))
 
         identity = const.tile([P, P], F32)
         make_identity(nc, identity[:])
+        swap = const.tile([P, P], F32)
+        nc.gpsimd.tensor_copy(out=swap[:, 0:HALF], in_=identity[:, HALF:D])
+        nc.gpsimd.tensor_copy(out=swap[:, HALF:D], in_=identity[:, 0:HALF])
+        identity_bf16 = const.tile([P, P], BF16)
+        make_identity(nc, identity_bf16[:])
 
         def transpose_tile(rows, grouped):
             words = rows.bitcast(F32)
@@ -92,57 +100,53 @@ def tile_attention_pa_kernel(tc, hidden_states, cos, sin, wq, wk, wv, out_0, out
                     )
             nc.scalar.copy(out=grouped, in_=bank[:].rearrange("p (g u r) -> p g r u", g=PASSES, u=2))
 
-        x_codes = mx_pool.tile([P, TOKEN_TILES * PASSES * P], U32, align_bytes=64)
-        x_scales = mx_pool.tile([P, TOKEN_TILES * PASSES * P], U8, align_bytes=64)
-
-        def transpose_x(tiles):
-            grouped = tile_grouped_pool.tile([P, len(tiles) * PASSES * P * 4], BF16, align_bytes=64)
-            view = grouped[:].bitcast(F32).rearrange("p (t g r u) -> p t g r u", t=len(tiles), g=PASSES, u=2)
-            for i, t in enumerate(tiles):
-                transpose_tile(x_raw[:, t, :], view[:, i])
-            return grouped
-
-        def quantise_x(tiles, grouped):
-            span = slice(tiles[0] * PASSES * P, (tiles[-1] + 1) * PASSES * P)
-            nc.vector.quantize_mx(out=x_codes[:, span].bitcast(FP8X4), scales=x_scales[:, span], in_=grouped[:])
-
         def mx_tiles(name):
             codes = mx_pool.tile([P, PASSES * CHUNK], U32, name=name + "_codes", align_bytes=64)
             scales = mx_pool.tile([P, PASSES * CHUNK], U8, name=name + "_scales", align_bytes=64)
             return codes, scales
 
-        def transpose_w(raw, tiles, pool):
-            columns = len(tiles) * P
-            grouped = pool.tile([P, PASSES * columns * 4], BF16, align_bytes=64)
-            view = grouped[:].bitcast(F32).rearrange("p (g c u) -> p g c u", g=PASSES, u=2)
-            for i, tile in enumerate(tiles):
-                transpose_tile(raw[:, tile, :], view[:, :, i * P : (i + 1) * P, :])
+        x_mx = [mx_tiles("x%d" % h) for h in range(2)]
+        w_mx = [mx_tiles("w%d" % n) for n in range(len(w_raw))]
+        v_mx = mx_tiles("v")
+
+        def one_tile(raw, i):
+            grouped = tile_grouped_pool.tile([P, PASSES * P * 4], BF16, align_bytes=64)
+            transpose_tile(raw[:, i, :], grouped[:].bitcast(F32).rearrange("p (g r u) -> p g r u", g=PASSES, u=2))
             return grouped
 
-        def quantise_w(weights, tiles, grouped):
-            codes, scales = weights
-            columns = len(tiles) * P
-            runs = 1 if columns == CHUNK else PASSES
-            width = PASSES * columns // runs
-            for g in range(runs):
-                first = g * CHUNK + tiles[0] * P
+        def quantise_tile(operand, i, grouped):
+            codes, scales = operand
+            for g in range(PASSES):
+                columns = slice(g * CHUNK + i * P, g * CHUNK + (i + 1) * P)
                 nc.vector.quantize_mx(
-                    out=codes[:, first : first + width].bitcast(FP8X4),
-                    scales=scales[:, first : first + width],
-                    in_=grouped[:, 4 * g * width : 4 * (g + 1) * width],
+                    out=codes[:, columns].bitcast(FP8X4),
+                    scales=scales[:, columns],
+                    in_=grouped[:, g * 4 * P : (g + 1) * 4 * P],
                 )
 
-        def project(bank, t, weights):
-            w_codes, w_scales = weights
+        def chunk_grouped():
+            grouped = w_grouped_pool.tile([P, PASSES * CHUNK * 4], BF16, align_bytes=64)
+            return grouped
+
+        def chunk_tiles(raw, tiles, grouped):
+            view = grouped[:].bitcast(F32).rearrange("p (g c u) -> p g c u", g=PASSES, u=2)
+            for i in tiles:
+                transpose_tile(raw[:, i, :], view[:, :, i * P : (i + 1) * P, :])
+
+        def quantise_chunk(operand, grouped):
+            codes, scales = operand
+            nc.vector.quantize_mx(out=codes[:].bitcast(FP8X4), scales=scales[:], in_=grouped[:])
+
+        def multiply(bank, stationary, i, moving):
             for g in range(PASSES):
-                tokens = slice((t * PASSES + g) * P, (t * PASSES + g + 1) * P)
-                features = slice(g * CHUNK, (g + 1) * CHUNK)
+                columns = slice(g * CHUNK + i * P, g * CHUNK + (i + 1) * P)
+                rows = slice(g * CHUNK, (g + 1) * CHUNK)
                 nc.tensor.matmul_mx(
                     out=bank[:],
-                    lhsT=x_codes[:, tokens].bitcast(FP8X4),
-                    lhsT_scale=x_scales[:, tokens],
-                    rhs=w_codes[:, features].bitcast(FP8X4),
-                    rhs_scale=w_scales[:, features],
+                    lhsT=stationary[0][:, columns].bitcast(FP8X4),
+                    lhsT_scale=stationary[1][:, columns],
+                    rhs=moving[0][:, rows].bitcast(FP8X4),
+                    rhs_scale=moving[1][:, rows],
                     start=(g == 0),
                     stop=(g == PASSES - 1),
                 )
@@ -156,8 +160,8 @@ def tile_attention_pa_kernel(tc, hidden_states, cos, sin, wq, wk, wv, out_0, out
             nc.vector.tensor_scalar_mul(out=rot[:, :, 1, 0, :], in0=tables[:, 1, :, 0:HALF], scalar1=-1.0)
 
         def products(prod, t, n):
-            acc = vector_banks.tile([P, CHUNK], F32)
-            project(acc, t, w_mx[n])
+            acc = vector_banks.tile([P, CHUNK], F32, tag="acc")
+            multiply(acc, x_mx[t // TILES], t % TILES, w_mx[n])
             nc.vector.tensor_tensor(
                 out=prod.rearrange("p h s (o j) -> p h s o j", o=2),
                 in0=acc[:]
@@ -177,16 +181,47 @@ def tile_attention_pa_kernel(tc, hidden_states, cos, sin, wq, wk, wv, out_0, out
                 in_=rotated.rearrange("p (t h) d -> p t (h d)", h=HEADS),
             )
 
-        grouped = transpose_x([0])
-        quantise_x([0], grouped)
-        w_mx = [mx_tiles("w%d" % n) for n in range(len(w_raw))]
-        v_mx = mx_tiles("v")
-        for i in range(TILES):
-            grouped = transpose_w(w_raw[0], [i], tile_grouped_pool)
-            quantise_w(w_mx[0], [i], grouped)
-        grouped = transpose_x([1])
-        quantise_x([1], grouped)
-        build_rotation()
+        turned = const.tile([P, 2, CHUNK], BF16)
+
+        def turn_tables():
+            flat = rot[:].rearrange("p t s o j -> p t (s o j)")
+            for a in range(2):
+                bank = scalar_banks.tile([P, CHUNK], BF16, tag="bank")
+                for i in range(TILES):
+                    t = TILES + i
+                    table = flat[:, t, HALF : HALF + D] if a else tables[:, 0, t, :]
+                    nc.tensor.transpose(bank[:, i * P : (i + 1) * P], table, identity_bf16[:])
+                nc.scalar.copy(out=turned[:, a, :], in_=bank[:])
+
+        def head_products(n, h):
+            acc = vector_banks.tile([P, CHUNK], F32, tag="acc")
+            multiply(acc, w_mx[n], h, x_mx[1])
+            prod = head_prod_pool.tile([P, 2, CHUNK], F32)
+            nc.vector.tensor_tensor(
+                out=prod[:], in0=acc[:].unsqueeze(1).to_broadcast([P, 2, CHUNK]), in1=turned[:], op=MULT
+            )
+            return prod
+
+        def head_sum(prod, block, h):
+            bank = scalar_banks.tile([P, TILES, D], F32, tag="bank")
+            for i in range(TILES):
+                for a, order in enumerate((identity, swap)):
+                    nc.tensor.matmul(
+                        bank[:, i, :],
+                        lhsT=prod[:, a, i * P : (i + 1) * P],
+                        rhs=order[:],
+                        is_transpose=True,
+                        start=(a == 0),
+                        stop=(a == 1),
+                    )
+            nc.scalar.copy(out=block[:, :, h * D : (h + 1) * D], in_=bank[:])
+
+        def new_block():
+            block = block_pool.tile([P, TILES, CHUNK], F32)
+            return block
+
+        def store_block(block, n):
+            nc.sync.dma_start(out=rotated_out[n][:, TILES:TOKEN_TILES, :], in_=block[:])
 
         plain_tiles = []
 
@@ -196,56 +231,109 @@ def tile_attention_pa_kernel(tc, hidden_states, cos, sin, wq, wk, wv, out_0, out
                 plain_tiles.append(plain)
             plain = plain_tiles[-1]
             bank = scalar_banks.tile([P, CHUNK], F32, tag="bank")
-            project(bank, t, v_mx)
+            multiply(bank, x_mx[t // TILES], t % TILES, v_mx)
             nc.scalar.copy(out=plain[:, t % 2, :], in_=bank[:])
             if t % 2 == 1:
                 nc.sync.dma_start(out=v_out[:, t - 1 : t + 1, :], in_=plain[:])
 
-        all_tiles = list(range(TILES))
-        last_chunk = len(w_raw) - 1
-        for n in range(len(w_raw)):
-            for t in range(TOKEN_TILES):
-                if t % 2 == 0:
-                    rotated = rotated_pool.tile([P, 2 * HEADS, D], F32)
-                    prod = prod_pool.tile([P, 2 * HEADS, 2, D], F32)
-                heads = slice((t % 2) * HEADS, (t % 2 + 1) * HEADS)
-                if n == 0 and t == 3:
-                    quantise_x([4, 5, 6, 7], x_grouped)
-                if n == 0 and t == 5:
-                    quantise_w(w_mx[1], all_tiles, w_grouped)
-                    quantise_w(w_mx[2], all_tiles, w_grouped_2)
-                products(prod[:, heads], t, n)
-                if n == 0:
-                    if t == 0:
-                        x_grouped = transpose_x([2])
-                        quantise_x([2], x_grouped)
-                    if t == 1:
-                        x_grouped = transpose_x([3])
-                        quantise_x([3], x_grouped)
-                        x_grouped = transpose_x([4, 5, 6, 7])
-                    if t == 2:
-                        w_grouped = transpose_w(w_raw[1], all_tiles, w_grouped_pool)
-                    if t == 4:
-                        w_grouped_2 = transpose_w(w_raw[2], all_tiles, w_grouped_pool)
-                if n == last_chunk and t >= TOKEN_TILES - 2:
-                    add(rotated[:, heads], prod[:, heads], nc.vector if t == TOKEN_TILES - 1 else nc.gpsimd)
-                    store(rotated[:, heads], n, t, t + 1)
-                elif t % 2 == 1:
-                    add(rotated[:], prod[:], nc.vector if n == 0 and t <= 3 else nc.gpsimd)
-                    store(rotated[:], n, t - 1, t + 1)
-                if n > 0:
-                    if n == 1 and t == 1:
-                        w_grouped = transpose_w(w_raw[3], all_tiles, w_grouped_pool)
-                    if n == 1 and t == 3:
-                        quantise_w(w_mx[3], all_tiles, w_grouped)
-                    if n == 1 and t == 5:
-                        w_grouped = transpose_w(w_raw[4], all_tiles, w_grouped_pool)
-                    if n == 1 and t == 7:
-                        quantise_w(w_mx[4], all_tiles, w_grouped)
-                    if n == 2 and t == 1:
-                        w_grouped = transpose_w(v_raw, all_tiles, w_grouped_pool)
-                    if n == 2 and t == 3:
-                        quantise_w(v_mx, all_tiles, w_grouped)
-                    slot = (n - 2) * TOKEN_TILES + t
-                    if slot >= 6 and slot % 2 == 0 and slot // 2 <= TOKEN_TILES + 2:
-                        plain_tile(slot // 2 - 3)
+        pairs = {}
+
+        def token_tile(n, t):
+            if t % 2 == 0:
+                rotated = rotated_pool.tile([P, 2 * HEADS, D], F32)
+                prod = prod_pool.tile([P, 2 * HEADS, 2, D], F32)
+                pairs[n, t // 2] = (rotated, prod)
+            products(pairs[n, t // 2][1][:, (t % 2) * HEADS : (t % 2 + 1) * HEADS], t, n)
+
+        def sum_pair(n, p, adder):
+            rotated, prod = pairs[n, p]
+            add(rotated[:], prod[:], adder)
+            store(rotated[:], n, 2 * p, 2 * p + 2)
+
+        def pair(n, p):
+            token_tile(n, 2 * p)
+            token_tile(n, 2 * p + 1)
+            sum_pair(n, p, nc.gpsimd)
+
+        def prepared(raw):
+            grouped = chunk_grouped()
+            chunk_tiles(raw, range(TILES), grouped)
+            return grouped
+
+        grouped = one_tile(x_raw[0], 0)
+        quantise_tile(x_mx[0], 0, grouped)
+        for i in range(TILES):
+            grouped = one_tile(w_raw[0], i)
+            quantise_tile(w_mx[0], i, grouped)
+        grouped = one_tile(x_raw[0], 1)
+        quantise_tile(x_mx[0], 1, grouped)
+        build_rotation()
+
+        token_tile(0, 0)
+        grouped = one_tile(x_raw[0], 2)
+        quantise_tile(x_mx[0], 2, grouped)
+        token_tile(0, 1)
+        grouped = one_tile(x_raw[0], 3)
+        quantise_tile(x_mx[0], 3, grouped)
+        sum_pair(0, 0, nc.vector)
+        x_grouped = prepared(x_raw[1])
+        token_tile(0, 2)
+        quantise_chunk(x_mx[1], x_grouped)
+        token_tile(0, 3)
+        sum_pair(0, 1, nc.gpsimd)
+        turn_tables()
+        w_grouped = chunk_grouped()
+        chunk_tiles(w_raw[1], (0, 1), w_grouped)
+        block = new_block()
+        prods = [head_products(0, 0), head_products(0, 1)]
+        chunk_tiles(w_raw[1], (2, 3), w_grouped)
+        quantise_chunk(w_mx[1], w_grouped)
+        prods += [head_products(0, 2), head_products(0, 3)]
+        for h in (0, 1):
+            head_sum(prods[h], block, h)
+        pair(1, 0)
+        for h in (2, 3):
+            head_sum(prods[h], block, h)
+        store_block(block, 0)
+        w_grouped = chunk_grouped()
+        chunk_tiles(w_raw[2], (0, 1), w_grouped)
+        block = new_block()
+        prods = [head_products(1, 0), head_products(1, 1)]
+        chunk_tiles(w_raw[2], (2, 3), w_grouped)
+        quantise_chunk(w_mx[2], w_grouped)
+        pair(1, 1)
+        for h in (0, 1):
+            head_sum(prods[h], block, h)
+        pair(2, 0)
+        w_grouped = prepared(w_raw[3])
+        pair(2, 1)
+        prods += [head_products(1, 2), head_products(1, 3)]
+        quantise_chunk(w_mx[3], w_grouped)
+        pair(2, 2)
+        for h in (2, 3):
+            head_sum(prods[h], block, h)
+        store_block(block, 1)
+        pair(2, 3)
+        w_grouped = prepared(v_raw)
+        pair(3, 0)
+        quantise_chunk(v_mx, w_grouped)
+        pair(3, 1)
+        w_grouped = prepared(w_raw[4])
+        pair(3, 2)
+        quantise_chunk(w_mx[4], w_grouped)
+        plain_tile(0)
+        plain_tile(1)
+        pair(3, 3)
+        plain_tile(2)
+        plain_tile(3)
+        for p in range(PAIRS - 1):
+            pair(4, p)
+            if p < 2:
+                plain_tile(4 + 2 * p)
+                plain_tile(5 + 2 * p)
+        for t in (TOKEN_TILES - 2, TOKEN_TILES - 1):
+            token_tile(4, t)
+            rotated, prod = pairs[4, PAIRS - 1]
+            heads = slice((t % 2) * HEADS, (t % 2 + 1) * HEADS)
+            add(rotated[:, heads], prod[:, heads], nc.vector if t == TOKEN_TILES - 1 else nc.gpsimd)
+            store(rotated[:, heads], 4, t, t + 1)

@@ -75,10 +75,11 @@ def tile_attention_pa_kernel(tc, hidden_states, cos, sin, wq, wk, wv, out_0, out
         nc.sync.dma_start(out=tables[:, 1], in_=sin.rearrange("(p t) o d -> p t (o d)", t=TOKEN_TILES))
         for t in range(2, TOKEN_TILES):
             load_x(t)
-        for n in range(1, Q_CHUNKS):
-            w_raw.append(load(rotated_rows[n], "w_raw%d" % n))
+        w_raw.append(load(rotated_rows[1], "w_raw1"))
+        w_raw.append(load(rotated_rows[2], "w_raw2"))
         v_raw = load(weight_rows(wv, 0), "v_raw")
-        w_raw.append(load(rotated_rows[Q_CHUNKS], "w_raw%d" % Q_CHUNKS))
+        w_raw.append(load(rotated_rows[3], "w_raw3"))
+        w_raw.append(load(rotated_rows[4], "w_raw4"))
 
         identity = const.tile([P, P], F32)
         make_identity(nc, identity[:])
@@ -216,12 +217,12 @@ def tile_attention_pa_kernel(tc, hidden_states, cos, sin, wq, wk, wv, out_0, out
                     )
             nc.scalar.copy(out=block[:, :, h * D : (h + 1) * D], in_=bank[:])
 
-        def new_block():
-            block = block_pool.tile([P, TILES, CHUNK], F32)
+        def new_block(heads):
+            block = block_pool.tile([P, TILES, heads * D], F32)
             return block
 
-        def store_block(block, n):
-            nc.sync.dma_start(out=rotated_out[n][:, TILES:TOKEN_TILES, :], in_=block[:])
+        def store_block(block, n, first, last):
+            nc.sync.dma_start(out=rotated_out[n][:, TILES:TOKEN_TILES, first * D : last * D], in_=block[:])
 
         plain_tiles = []
 
@@ -281,59 +282,64 @@ def tile_attention_pa_kernel(tc, hidden_states, cos, sin, wq, wk, wv, out_0, out
         quantise_chunk(x_mx[1], x_grouped)
         token_tile(0, 3)
         sum_pair(0, 1, nc.gpsimd)
-        turn_tables()
         w_grouped = chunk_grouped()
-        chunk_tiles(w_raw[1], (0, 1), w_grouped)
-        block = new_block()
-        prods = [head_products(0, 0), head_products(0, 1)]
-        chunk_tiles(w_raw[1], (2, 3), w_grouped)
+        chunk_tiles(w_raw[1], (0, 1, 2), w_grouped)
+        token_tile(0, 4)
+        token_tile(0, 5)
+        chunk_tiles(w_raw[1], (3,), w_grouped)
         quantise_chunk(w_mx[1], w_grouped)
-        prods += [head_products(0, 2), head_products(0, 3)]
-        for h in (0, 1):
-            head_sum(prods[h], block, h)
+        sum_pair(0, 2, nc.gpsimd)
+        pair(0, 3)
         pair(1, 0)
-        for h in (2, 3):
-            head_sum(prods[h], block, h)
-        store_block(block, 0)
-        w_grouped = chunk_grouped()
-        chunk_tiles(w_raw[2], (0, 1), w_grouped)
-        block = new_block()
-        prods = [head_products(1, 0), head_products(1, 1)]
-        chunk_tiles(w_raw[2], (2, 3), w_grouped)
-        quantise_chunk(w_mx[2], w_grouped)
+        w_grouped = prepared(w_raw[2])
         pair(1, 1)
-        for h in (0, 1):
-            head_sum(prods[h], block, h)
-        pair(2, 0)
+        token_tile(1, 4)
+        token_tile(1, 5)
+        quantise_chunk(w_mx[2], w_grouped)
+        sum_pair(1, 2, nc.gpsimd)
+        v_grouped = prepared(v_raw)
+        pair(1, 3)
+        token_tile(2, 0)
+        token_tile(2, 1)
+        quantise_chunk(v_mx, v_grouped)
+        sum_pair(2, 0, nc.gpsimd)
         w_grouped = prepared(w_raw[3])
         pair(2, 1)
-        prods += [head_products(1, 2), head_products(1, 3)]
-        quantise_chunk(w_mx[3], w_grouped)
-        pair(2, 2)
-        for h in (2, 3):
-            head_sum(prods[h], block, h)
-        store_block(block, 1)
-        pair(2, 3)
-        w_grouped = prepared(v_raw)
-        pair(3, 0)
-        quantise_chunk(v_mx, w_grouped)
-        pair(3, 1)
-        w_grouped = prepared(w_raw[4])
-        pair(3, 2)
-        quantise_chunk(w_mx[4], w_grouped)
         plain_tile(0)
         plain_tile(1)
-        pair(3, 3)
+        token_tile(2, 4)
+        token_tile(2, 5)
+        quantise_chunk(w_mx[3], w_grouped)
+        sum_pair(2, 2, nc.gpsimd)
         plain_tile(2)
         plain_tile(3)
-        for p in range(PAIRS - 1):
-            pair(4, p)
-            if p < 2:
-                plain_tile(4 + 2 * p)
-                plain_tile(5 + 2 * p)
-        for t in (TOKEN_TILES - 2, TOKEN_TILES - 1):
+        turn_tables()
+        pair(2, 3)
+        pair(3, 0)
+        w_grouped = prepared(w_raw[4])
+        block = new_block(2)
+        prods = [head_products(3, 0), head_products(3, 1)]
+        quantise_chunk(w_mx[4], w_grouped)
+        pair(3, 1)
+        for h in (0, 1):
+            head_sum(prods[h], block, h)
+        store_block(block, 3, 0, 2)
+        plain_tile(4)
+        plain_tile(5)
+        pair(4, 0)
+        plain_tile(6)
+        plain_tile(7)
+        pair(4, 1)
+        pair(4, 2)
+        prods = [head_products(3, 2), head_products(3, 3)]
+        for t in (6, 7):
             token_tile(4, t)
-            rotated, prod = pairs[4, PAIRS - 1]
+        block = new_block(2)
+        for h in (0, 1):
+            head_sum(prods[h], block, h)
+        store_block(block, 3, 2, 4)
+        for t in (6, 7):
+            rotated, prod = pairs[4, 3]
             heads = slice((t % 2) * HEADS, (t % 2 + 1) * HEADS)
-            add(rotated[:, heads], prod[:, heads], nc.vector if t == TOKEN_TILES - 1 else nc.gpsimd)
+            add(rotated[:, heads], prod[:, heads], nc.vector if t == 7 else nc.gpsimd)
             store(rotated[:, heads], 4, t, t + 1)

@@ -24,6 +24,7 @@ D = 128
 HALF = D // 2
 HEADS = CHUNK // D
 Q_CHUNKS = 4
+FIRST_TABLES = 2
 
 FLOPS = 2 * 1024 * 1024 * 3072
 
@@ -67,13 +68,20 @@ def tile_attention_pa_kernel(tc, hidden_states, cos, sin, wq, wk, wv, out_0, out
         def load_x(t):
             nc.sync.dma_start(out=x_raw[t // TILES][:, t % TILES, :], in_=x_rows[:, t, :])
 
+        tables = const.tile([P, 2, TOKEN_TILES, D], BF16)
+
+        def load_tables(first, last):
+            for a, table in enumerate((cos, sin)):
+                rows = table.rearrange("(p t) o d -> p t (o d)", t=TOKEN_TILES)
+                nc.sync.dma_start(out=tables[:, a, first:last], in_=rows[:, first:last, :])
+
         load_x(0)
         w_raw = [load(rotated_rows[0], "w_raw0")]
+        load_tables(0, FIRST_TABLES)
         load_x(1)
-        tables = const.tile([P, 2, TOKEN_TILES, D], BF16)
-        nc.sync.dma_start(out=tables[:, 0], in_=cos.rearrange("(p t) o d -> p t (o d)", t=TOKEN_TILES))
-        nc.sync.dma_start(out=tables[:, 1], in_=sin.rearrange("(p t) o d -> p t (o d)", t=TOKEN_TILES))
-        for t in range(2, TOKEN_TILES):
+        load_x(2)
+        load_tables(FIRST_TABLES, TOKEN_TILES)
+        for t in range(3, TOKEN_TILES):
             load_x(t)
         w_raw.append(load(rotated_rows[1], "w_raw1"))
         w_raw.append(load(rotated_rows[2], "w_raw2"))
@@ -115,7 +123,19 @@ def tile_attention_pa_kernel(tc, hidden_states, cos, sin, wq, wk, wv, out_0, out
             transpose_tile(raw[:, i, :], grouped[:].bitcast(F32).rearrange("p (g r u) -> p g r u", g=PASSES, u=2))
             return grouped
 
-        def quantise_tile(operand, i, grouped):
+        def token_columns(t, g):
+            if t < TILES:
+                first = (PASSES * t + g) * P
+            else:
+                first = g * CHUNK + (t - TILES) * P
+            return slice(first, first + P)
+
+        def quantise_token_tile(t, grouped):
+            codes, scales = x_mx[0]
+            columns = slice(PASSES * t * P, PASSES * (t + 1) * P)
+            nc.vector.quantize_mx(out=codes[:, columns].bitcast(FP8X4), scales=scales[:, columns], in_=grouped[:])
+
+        def quantise_weight_tile(operand, i, grouped):
             codes, scales = operand
             for g in range(PASSES):
                 columns = slice(g * CHUNK + i * P, g * CHUNK + (i + 1) * P)
@@ -138,9 +158,9 @@ def tile_attention_pa_kernel(tc, hidden_states, cos, sin, wq, wk, wv, out_0, out
             codes, scales = operand
             nc.vector.quantize_mx(out=codes[:].bitcast(FP8X4), scales=scales[:], in_=grouped[:])
 
-        def multiply(bank, stationary, i, moving):
+        def multiply(bank, stationary, columns_of, moving):
             for g in range(PASSES):
-                columns = slice(g * CHUNK + i * P, g * CHUNK + (i + 1) * P)
+                columns = columns_of(g)
                 rows = slice(g * CHUNK, (g + 1) * CHUNK)
                 nc.tensor.matmul_mx(
                     out=bank[:],
@@ -154,15 +174,19 @@ def tile_attention_pa_kernel(tc, hidden_states, cos, sin, wq, wk, wv, out_0, out
 
         rot = const.tile([P, TOKEN_TILES, 2, 2, HALF], BF16)
 
-        def build_rotation():
-            nc.vector.tensor_copy(out=rot[:, :, 0, 0, :], in_=tables[:, 0, :, 0:HALF])
-            nc.vector.tensor_copy(out=rot[:, :, 1, 1, :], in_=tables[:, 0, :, HALF:D])
-            nc.vector.tensor_copy(out=rot[:, :, 0, 1, :], in_=tables[:, 1, :, HALF:D])
-            nc.vector.tensor_scalar_mul(out=rot[:, :, 1, 0, :], in0=tables[:, 1, :, 0:HALF], scalar1=-1.0)
+        def build_rotation(first, last, copy, multiply_by):
+            tokens = slice(first, last)
+            copy(out=rot[:, tokens, 0, 0, :], in_=tables[:, 0, tokens, 0:HALF])
+            copy(out=rot[:, tokens, 1, 1, :], in_=tables[:, 0, tokens, HALF:D])
+            copy(out=rot[:, tokens, 0, 1, :], in_=tables[:, 1, tokens, HALF:D])
+            multiply_by(rot[:, tokens, 1, 0, :], tables[:, 1, tokens, 0:HALF], -1.0)
 
-        def products(prod, t, n):
+        def project(n, t):
             acc = vector_banks.tile([P, CHUNK], F32, tag="acc")
-            multiply(acc, x_mx[t // TILES], t % TILES, w_mx[n])
+            multiply(acc, x_mx[t // TILES], lambda g: token_columns(t, g), w_mx[n])
+            return acc
+
+        def products(prod, t, acc):
             nc.vector.tensor_tensor(
                 out=prod.rearrange("p h s (o j) -> p h s o j", o=2),
                 in0=acc[:]
@@ -196,7 +220,7 @@ def tile_attention_pa_kernel(tc, hidden_states, cos, sin, wq, wk, wv, out_0, out
 
         def head_products(n, h):
             acc = vector_banks.tile([P, CHUNK], F32, tag="acc")
-            multiply(acc, w_mx[n], h, x_mx[1])
+            multiply(acc, w_mx[n], lambda g: slice(g * CHUNK + h * P, g * CHUNK + (h + 1) * P), x_mx[1])
             prod = head_prod_pool.tile([P, 2, CHUNK], F32)
             nc.vector.tensor_tensor(
                 out=prod[:], in0=acc[:].unsqueeze(1).to_broadcast([P, 2, CHUNK]), in1=turned[:], op=MULT
@@ -232,19 +256,22 @@ def tile_attention_pa_kernel(tc, hidden_states, cos, sin, wq, wk, wv, out_0, out
                 plain_tiles.append(plain)
             plain = plain_tiles[-1]
             bank = scalar_banks.tile([P, CHUNK], F32, tag="bank")
-            multiply(bank, x_mx[t // TILES], t % TILES, v_mx)
+            multiply(bank, x_mx[t // TILES], lambda g: token_columns(t, g), v_mx)
             nc.scalar.copy(out=plain[:, t % 2, :], in_=bank[:])
             if t % 2 == 1:
                 nc.sync.dma_start(out=v_out[:, t - 1 : t + 1, :], in_=plain[:])
 
         pairs = {}
 
-        def token_tile(n, t):
+        def rotate(n, t, acc):
             if t % 2 == 0:
                 rotated = rotated_pool.tile([P, 2 * HEADS, D], F32)
                 prod = prod_pool.tile([P, 2 * HEADS, 2, D], F32)
                 pairs[n, t // 2] = (rotated, prod)
-            products(pairs[n, t // 2][1][:, (t % 2) * HEADS : (t % 2 + 1) * HEADS], t, n)
+            products(pairs[n, t // 2][1][:, (t % 2) * HEADS : (t % 2 + 1) * HEADS], t, acc)
+
+        def token_tile(n, t):
+            rotate(n, t, project(n, t))
 
         def sum_pair(n, p, adder):
             rotated, prod = pairs[n, p]
@@ -262,25 +289,31 @@ def tile_attention_pa_kernel(tc, hidden_states, cos, sin, wq, wk, wv, out_0, out
             return grouped
 
         grouped = one_tile(x_raw[0], 0)
-        quantise_tile(x_mx[0], 0, grouped)
+        quantise_token_tile(0, grouped)
         for i in range(TILES):
             grouped = one_tile(w_raw[0], i)
-            quantise_tile(w_mx[0], i, grouped)
+            quantise_weight_tile(w_mx[0], i, grouped)
+        build_rotation(0, FIRST_TABLES, nc.vector.tensor_copy, nc.vector.tensor_scalar_mul)
         grouped = one_tile(x_raw[0], 1)
-        quantise_tile(x_mx[0], 1, grouped)
-        build_rotation()
+        quantise_token_tile(1, grouped)
+        grouped2 = one_tile(x_raw[0], 2)
+        build_rotation(FIRST_TABLES, TOKEN_TILES, nc.scalar.copy, nc.scalar.mul)
 
-        token_tile(0, 0)
-        grouped = one_tile(x_raw[0], 2)
-        quantise_tile(x_mx[0], 2, grouped)
-        token_tile(0, 1)
-        grouped = one_tile(x_raw[0], 3)
-        quantise_tile(x_mx[0], 3, grouped)
+        accs = [project(0, 0), project(0, 1)]
+        rotate(0, 0, accs[0])
+        quantise_token_tile(2, grouped2)
+        grouped3 = one_tile(x_raw[0], 3)
+        rotate(0, 1, accs[1])
+        quantise_token_tile(3, grouped3)
+        x_grouped = chunk_grouped()
+        chunk_tiles(x_raw[1], (0,), x_grouped)
+        accs = [project(0, 2)]
+        chunk_tiles(x_raw[1], (1, 2, 3), x_grouped)
+        accs.append(project(0, 3))
+        rotate(0, 2, accs[0])
         sum_pair(0, 0, nc.vector)
-        x_grouped = prepared(x_raw[1])
-        token_tile(0, 2)
         quantise_chunk(x_mx[1], x_grouped)
-        token_tile(0, 3)
+        rotate(0, 3, accs[1])
         sum_pair(0, 1, nc.gpsimd)
         w_grouped = chunk_grouped()
         chunk_tiles(w_raw[1], (0, 1, 2), w_grouped)

@@ -18,6 +18,7 @@ PASSES = K // K_PASS
 WORDS = K // 2
 TILES = 4
 CHUNK = TILES * P
+HALF_CHUNK = CHUNK // 2
 TOKEN_TILES = 8
 PAIRS = TOKEN_TILES // 2
 D = 128
@@ -38,10 +39,11 @@ def tile_attention_pa_kernel(tc, hidden_states, cos, sin, wq, wk, wv, out_0, out
         mx_pool = ctx.enter_context(tc.tile_pool(name="mx", bufs=1))
         tile_grouped_pool = ctx.enter_context(tc.tile_pool(name="tile_grouped", bufs=4))
         head_prod_pool = ctx.enter_context(tc.tile_pool(name="head_prod", bufs=4))
+        half_grouped_pool = ctx.enter_context(tc.tile_pool(name="half_grouped", bufs=2))
         block_pool = ctx.enter_context(tc.tile_pool(name="block", bufs=2))
-        w_grouped_pool = ctx.enter_context(tc.tile_pool(name="w_grouped", bufs=2))
+        w_grouped_pool = ctx.enter_context(tc.tile_pool(name="w_grouped", bufs=3))
         prod_pool = ctx.enter_context(tc.tile_pool(name="prod", bufs=4))
-        rotated_pool = ctx.enter_context(tc.tile_pool(name="rotated", bufs=5))
+        rotated_pool = ctx.enter_context(tc.tile_pool(name="rotated", bufs=3))
         plain_pool = ctx.enter_context(tc.tile_pool(name="plain", bufs=3))
         scalar_banks = ctx.enter_context(tc.psum_pool(name="scalar_banks", bufs=4))
         vector_banks = ctx.enter_context(tc.psum_pool(name="vector_banks", bufs=4))
@@ -127,7 +129,8 @@ def tile_attention_pa_kernel(tc, hidden_states, cos, sin, wq, wk, wv, out_0, out
             if t < TILES:
                 first = (PASSES * t + g) * P
             else:
-                first = g * CHUNK + (t - TILES) * P
+                half, i = divmod(t - TILES, TILES // 2)
+                first = (half * PASSES + g) * HALF_CHUNK + i * P
             return slice(first, first + P)
 
         def quantise_token_tile(t, grouped):
@@ -145,18 +148,34 @@ def tile_attention_pa_kernel(tc, hidden_states, cos, sin, wq, wk, wv, out_0, out
                     in_=grouped[:, g * 4 * P : (g + 1) * 4 * P],
                 )
 
+        def half_grouped():
+            grouped = half_grouped_pool.tile([P, PASSES * HALF_CHUNK * 2], F32, align_bytes=64)
+            return grouped
+
+        def half_tiles(half, grouped):
+            view = grouped[:].rearrange("p (g c u) -> p g c u", g=PASSES, u=2)
+            for i in range(TILES // 2):
+                transpose_tile(x_raw[1][:, half * (TILES // 2) + i, :], view[:, :, i * P : (i + 1) * P, :])
+
+        def quantise_half(half, grouped):
+            codes, scales = x_mx[1]
+            columns = slice(half * PASSES * HALF_CHUNK, (half + 1) * PASSES * HALF_CHUNK)
+            nc.vector.quantize_mx(
+                out=codes[:, columns].bitcast(FP8X4), scales=scales[:, columns], in_=grouped[:].bitcast(BF16)
+            )
+
         def chunk_grouped():
-            grouped = w_grouped_pool.tile([P, PASSES * CHUNK * 4], BF16, align_bytes=64)
+            grouped = w_grouped_pool.tile([P, PASSES * CHUNK * 2], F32, align_bytes=64)
             return grouped
 
         def chunk_tiles(raw, tiles, grouped):
-            view = grouped[:].bitcast(F32).rearrange("p (g c u) -> p g c u", g=PASSES, u=2)
+            view = grouped[:].rearrange("p (g c u) -> p g c u", g=PASSES, u=2)
             for i in tiles:
                 transpose_tile(raw[:, i, :], view[:, :, i * P : (i + 1) * P, :])
 
         def quantise_chunk(operand, grouped):
             codes, scales = operand
-            nc.vector.quantize_mx(out=codes[:].bitcast(FP8X4), scales=scales[:], in_=grouped[:])
+            nc.vector.quantize_mx(out=codes[:].bitcast(FP8X4), scales=scales[:], in_=grouped[:].bitcast(BF16))
 
         def multiply(bank, stationary, columns_of, moving):
             for g in range(PASSES):
@@ -168,6 +187,20 @@ def tile_attention_pa_kernel(tc, hidden_states, cos, sin, wq, wk, wv, out_0, out
                     lhsT_scale=stationary[1][:, columns],
                     rhs=moving[0][:, rows].bitcast(FP8X4),
                     rhs_scale=moving[1][:, rows],
+                    start=(g == 0),
+                    stop=(g == PASSES - 1),
+                )
+
+        def multiply_half(bank, stationary, h, half):
+            for g in range(PASSES):
+                columns = slice(g * CHUNK + h * P, g * CHUNK + (h + 1) * P)
+                tokens = slice((half * PASSES + g) * HALF_CHUNK, (half * PASSES + g + 1) * HALF_CHUNK)
+                nc.tensor.matmul_mx(
+                    out=bank,
+                    lhsT=stationary[0][:, columns].bitcast(FP8X4),
+                    lhsT_scale=stationary[1][:, columns],
+                    rhs=x_mx[1][0][:, tokens].bitcast(FP8X4),
+                    rhs_scale=x_mx[1][1][:, tokens],
                     start=(g == 0),
                     stop=(g == PASSES - 1),
                 )
@@ -220,7 +253,8 @@ def tile_attention_pa_kernel(tc, hidden_states, cos, sin, wq, wk, wv, out_0, out
 
         def head_products(n, h):
             acc = vector_banks.tile([P, CHUNK], F32, tag="acc")
-            multiply(acc, w_mx[n], lambda g: slice(g * CHUNK + h * P, g * CHUNK + (h + 1) * P), x_mx[1])
+            for half in range(2):
+                multiply_half(acc[:, half * HALF_CHUNK : (half + 1) * HALF_CHUNK], w_mx[n], h, half)
             prod = head_prod_pool.tile([P, 2, CHUNK], F32)
             nc.vector.tensor_tensor(
                 out=prod[:], in0=acc[:].unsqueeze(1).to_broadcast([P, 2, CHUNK]), in1=turned[:], op=MULT
@@ -265,18 +299,22 @@ def tile_attention_pa_kernel(tc, hidden_states, cos, sin, wq, wk, wv, out_0, out
 
         def rotate(n, t, acc):
             if t % 2 == 0:
-                rotated = rotated_pool.tile([P, 2 * HEADS, D], F32)
                 prod = prod_pool.tile([P, 2 * HEADS, 2, D], F32)
-                pairs[n, t // 2] = (rotated, prod)
-            products(pairs[n, t // 2][1][:, (t % 2) * HEADS : (t % 2 + 1) * HEADS], t, acc)
+                pairs[n, t // 2] = prod
+            products(pairs[n, t // 2][:, (t % 2) * HEADS : (t % 2 + 1) * HEADS], t, acc)
 
         def token_tile(n, t):
             rotate(n, t, project(n, t))
 
         def sum_pair(n, p, adder):
-            rotated, prod = pairs[n, p]
-            add(rotated[:], prod[:], adder)
+            rotated = rotated_pool.tile([P, 2 * HEADS, D], F32)
+            add(rotated[:], pairs[n, p][:], adder)
             store(rotated[:], n, 2 * p, 2 * p + 2)
+
+        def sum_pair_behind_quantise(n, p, grouped):
+            rotated = grouped[:, 0 : 2 * HEADS * D].rearrange("p (h d) -> p h d", d=D)
+            add(rotated, pairs[n, p][:], nc.gpsimd)
+            store(rotated, n, 2 * p, 2 * p + 2)
 
         def pair(n, p):
             token_tile(n, 2 * p)
@@ -305,23 +343,23 @@ def tile_attention_pa_kernel(tc, hidden_states, cos, sin, wq, wk, wv, out_0, out
         grouped3 = one_tile(x_raw[0], 3)
         rotate(0, 1, accs[1])
         quantise_token_tile(3, grouped3)
-        x_grouped = chunk_grouped()
-        chunk_tiles(x_raw[1], (0,), x_grouped)
-        accs = [project(0, 2)]
-        chunk_tiles(x_raw[1], (1, 2, 3), x_grouped)
-        accs.append(project(0, 3))
+        x_halves = [half_grouped(), half_grouped()]
+        half_tiles(0, x_halves[0])
+        accs = [project(0, 2), project(0, 3)]
+        half_tiles(1, x_halves[1])
+        quantise_half(0, x_halves[0])
+        sum_pair_behind_quantise(0, 0, x_halves[0])
         rotate(0, 2, accs[0])
-        sum_pair(0, 0, nc.vector)
-        quantise_chunk(x_mx[1], x_grouped)
         rotate(0, 3, accs[1])
-        sum_pair(0, 1, nc.gpsimd)
+        accs = [project(0, 4), project(0, 5)]
+        quantise_half(1, x_halves[1])
+        sum_pair_behind_quantise(0, 1, x_halves[1])
         w_grouped = chunk_grouped()
-        chunk_tiles(w_raw[1], (0, 1, 2), w_grouped)
-        token_tile(0, 4)
-        token_tile(0, 5)
-        chunk_tiles(w_raw[1], (3,), w_grouped)
+        chunk_tiles(w_raw[1], range(TILES), w_grouped)
+        rotate(0, 4, accs[0])
+        rotate(0, 5, accs[1])
         quantise_chunk(w_mx[1], w_grouped)
-        sum_pair(0, 2, nc.gpsimd)
+        sum_pair_behind_quantise(0, 2, w_grouped)
         pair(0, 3)
         pair(1, 0)
         w_grouped = prepared(w_raw[2])
@@ -329,13 +367,13 @@ def tile_attention_pa_kernel(tc, hidden_states, cos, sin, wq, wk, wv, out_0, out
         token_tile(1, 4)
         token_tile(1, 5)
         quantise_chunk(w_mx[2], w_grouped)
-        sum_pair(1, 2, nc.gpsimd)
+        sum_pair_behind_quantise(1, 2, w_grouped)
         v_grouped = prepared(v_raw)
         pair(1, 3)
         token_tile(2, 0)
         token_tile(2, 1)
         quantise_chunk(v_mx, v_grouped)
-        sum_pair(2, 0, nc.gpsimd)
+        sum_pair_behind_quantise(2, 0, v_grouped)
         w_grouped = prepared(w_raw[3])
         pair(2, 1)
         plain_tile(0)
@@ -343,7 +381,7 @@ def tile_attention_pa_kernel(tc, hidden_states, cos, sin, wq, wk, wv, out_0, out
         token_tile(2, 4)
         token_tile(2, 5)
         quantise_chunk(w_mx[3], w_grouped)
-        sum_pair(2, 2, nc.gpsimd)
+        sum_pair_behind_quantise(2, 2, w_grouped)
         plain_tile(2)
         plain_tile(3)
         turn_tables()
@@ -371,8 +409,8 @@ def tile_attention_pa_kernel(tc, hidden_states, cos, sin, wq, wk, wv, out_0, out
         for h in (0, 1):
             head_sum(prods[h], block, h)
         store_block(block, 3, 2, 4)
+        rotated = rotated_pool.tile([P, 2 * HEADS, D], F32)
         for t in (6, 7):
-            rotated, prod = pairs[4, 3]
             heads = slice((t % 2) * HEADS, (t % 2 + 1) * HEADS)
-            add(rotated[:, heads], prod[:, heads], nc.vector if t == 7 else nc.gpsimd)
+            add(rotated[:, heads], pairs[4, 3][:, heads], nc.vector if t == 7 else nc.gpsimd)
             store(rotated[:, heads], 4, t, t + 1)

@@ -20,10 +20,10 @@ TILES = 4
 CHUNK = TILES * P
 HALF_CHUNK = CHUNK // 2
 TOKEN_TILES = 8
-PAIRS = TOKEN_TILES // 2
 D = 128
 HALF = D // 2
 HEADS = CHUNK // D
+GROUP = 4
 Q_CHUNKS = 4
 FIRST_TABLES = 2
 
@@ -35,15 +35,15 @@ def tile_attention_pa_kernel(tc, hidden_states, cos, sin, wq, wk, wv, out_0, out
     with ExitStack() as ctx:
         ctx.enter_context(tc.manual_schedule())
         const = ctx.enter_context(tc.tile_pool(name="const", bufs=1))
-        raw_pool = ctx.enter_context(tc.tile_pool(name="raw", bufs=1))
+        raw_pool = ctx.enter_context(tc.tile_pool(name="raw", bufs=5))
         mx_pool = ctx.enter_context(tc.tile_pool(name="mx", bufs=1))
         tile_grouped_pool = ctx.enter_context(tc.tile_pool(name="tile_grouped", bufs=4))
-        head_prod_pool = ctx.enter_context(tc.tile_pool(name="head_prod", bufs=4))
+        head_prod_pool = ctx.enter_context(tc.tile_pool(name="head_prod", bufs=2))
         half_grouped_pool = ctx.enter_context(tc.tile_pool(name="half_grouped", bufs=2))
         block_pool = ctx.enter_context(tc.tile_pool(name="block", bufs=2))
         w_grouped_pool = ctx.enter_context(tc.tile_pool(name="w_grouped", bufs=3))
-        prod_pool = ctx.enter_context(tc.tile_pool(name="prod", bufs=4))
-        rotated_pool = ctx.enter_context(tc.tile_pool(name="rotated", bufs=3))
+        prod_pool = ctx.enter_context(tc.tile_pool(name="prod", bufs=3))
+        rotated_pool = ctx.enter_context(tc.tile_pool(name="rotated", bufs=4))
         plain_pool = ctx.enter_context(tc.tile_pool(name="plain", bufs=3))
         scalar_banks = ctx.enter_context(tc.psum_pool(name="scalar_banks", bufs=4))
         vector_banks = ctx.enter_context(tc.psum_pool(name="vector_banks", bufs=4))
@@ -59,13 +59,13 @@ def tile_attention_pa_kernel(tc, hidden_states, cos, sin, wq, wk, wv, out_0, out
         rotated_rows = [weight_rows(wq, c) for c in range(Q_CHUNKS)] + [weight_rows(wk, 0)]
         rotated_out = [q_out[:, :, c * CHUNK : (c + 1) * CHUNK] for c in range(Q_CHUNKS)] + [k_out]
 
-        def load(rows, name):
-            raw = raw_pool.tile([P, TILES, K], BF16, name=name)
+        def load(rows):
+            raw = raw_pool.tile([P, TILES, K], BF16, tag="raw")
             for i in range(TILES):
                 nc.sync.dma_start(out=raw[:, i, :], in_=rows[:, i, :])
             return raw
 
-        x_raw = [raw_pool.tile([P, TILES, K], BF16, name="x_raw%d" % h) for h in range(2)]
+        x_raw = [raw_pool.tile([P, TILES, K], BF16, name="x_raw%d" % h, tag="raw") for h in range(2)]
 
         def load_x(t):
             nc.sync.dma_start(out=x_raw[t // TILES][:, t % TILES, :], in_=x_rows[:, t, :])
@@ -78,18 +78,15 @@ def tile_attention_pa_kernel(tc, hidden_states, cos, sin, wq, wk, wv, out_0, out
                 nc.sync.dma_start(out=tables[:, a, first:last], in_=rows[:, first:last, :])
 
         load_x(0)
-        w_raw = [load(rotated_rows[0], "w_raw0")]
+        w_raw = [load(rotated_rows[0])]
         load_tables(0, FIRST_TABLES)
         load_x(1)
         load_x(2)
         load_tables(FIRST_TABLES, TOKEN_TILES)
         for t in range(3, TOKEN_TILES):
             load_x(t)
-        w_raw.append(load(rotated_rows[1], "w_raw1"))
-        w_raw.append(load(rotated_rows[2], "w_raw2"))
-        v_raw = load(weight_rows(wv, 0), "v_raw")
-        w_raw.append(load(rotated_rows[3], "w_raw3"))
-        w_raw.append(load(rotated_rows[4], "w_raw4"))
+        w_raw.append(load(rotated_rows[1]))
+        w_raw.append(load(rotated_rows[2]))
 
         identity = const.tile([P, P], F32)
         make_identity(nc, identity[:])
@@ -117,7 +114,7 @@ def tile_attention_pa_kernel(tc, hidden_states, cos, sin, wq, wk, wv, out_0, out
             return codes, scales
 
         x_mx = [mx_tiles("x%d" % h) for h in range(2)]
-        w_mx = [mx_tiles("w%d" % n) for n in range(len(w_raw))]
+        w_mx = [mx_tiles("w%d" % n) for n in range(len(rotated_rows))]
         v_mx = mx_tiles("v")
 
         def one_tile(raw, i):
@@ -295,31 +292,35 @@ def tile_attention_pa_kernel(tc, hidden_states, cos, sin, wq, wk, wv, out_0, out
             if t % 2 == 1:
                 nc.sync.dma_start(out=v_out[:, t - 1 : t + 1, :], in_=plain[:])
 
-        pairs = {}
+        groups = []
+
+        def new_group():
+            prod = prod_pool.tile([P, GROUP * HEADS, 2, D], F32)
+            groups.append((prod, []))
 
         def rotate(n, t, acc):
-            if t % 2 == 0:
-                prod = prod_pool.tile([P, 2 * HEADS, 2, D], F32)
-                pairs[n, t // 2] = prod
-            products(pairs[n, t // 2][:, (t % 2) * HEADS : (t % 2 + 1) * HEADS], t, acc)
+            prod, members = groups[-1]
+            first = len(members) * HEADS
+            products(prod[:, first : first + HEADS], t, acc)
+            members.append((n, t))
 
         def token_tile(n, t):
             rotate(n, t, project(n, t))
 
-        def sum_pair(n, p, adder):
+        def sum_group(rotated):
+            prod, members = groups[-1]
+            add(rotated, prod[:, 0 : len(members) * HEADS], nc.gpsimd)
+            for i in range(0, len(members), 2):
+                n, t = members[i]
+                store(rotated[:, i * HEADS : (i + 2) * HEADS], n, t, t + 2)
+
+        def sum_behind_quantise(grouped):
+            width = len(groups[-1][1]) * HEADS * D
+            sum_group(grouped[:, 0:width].rearrange("p (h d) -> p h d", d=D))
+
+        def sum_pair():
             rotated = rotated_pool.tile([P, 2 * HEADS, D], F32)
-            add(rotated[:], pairs[n, p][:], adder)
-            store(rotated[:], n, 2 * p, 2 * p + 2)
-
-        def sum_pair_behind_quantise(n, p, grouped):
-            rotated = grouped[:, 0 : 2 * HEADS * D].rearrange("p (h d) -> p h d", d=D)
-            add(rotated, pairs[n, p][:], nc.gpsimd)
-            store(rotated, n, 2 * p, 2 * p + 2)
-
-        def pair(n, p):
-            token_tile(n, 2 * p)
-            token_tile(n, 2 * p + 1)
-            sum_pair(n, p, nc.gpsimd)
+            sum_group(rotated[:])
 
         def prepared(raw):
             grouped = chunk_grouped()
@@ -338,79 +339,116 @@ def tile_attention_pa_kernel(tc, hidden_states, cos, sin, wq, wk, wv, out_0, out
         build_rotation(FIRST_TABLES, TOKEN_TILES, nc.scalar.copy, nc.scalar.mul)
 
         accs = [project(0, 0), project(0, 1)]
+        new_group()
         rotate(0, 0, accs[0])
         quantise_token_tile(2, grouped2)
         grouped3 = one_tile(x_raw[0], 3)
+        v_raw = load(weight_rows(wv, 0))
         rotate(0, 1, accs[1])
         quantise_token_tile(3, grouped3)
         x_halves = [half_grouped(), half_grouped()]
         half_tiles(0, x_halves[0])
         accs = [project(0, 2), project(0, 3)]
         half_tiles(1, x_halves[1])
+        w_raw.append(load(rotated_rows[3]))
+        w_raw.append(load(rotated_rows[4]))
         quantise_half(0, x_halves[0])
-        sum_pair_behind_quantise(0, 0, x_halves[0])
+        sum_behind_quantise(x_halves[0])
+        new_group()
         rotate(0, 2, accs[0])
         rotate(0, 3, accs[1])
         accs = [project(0, 4), project(0, 5)]
         quantise_half(1, x_halves[1])
-        sum_pair_behind_quantise(0, 1, x_halves[1])
+        sum_behind_quantise(x_halves[1])
         w_grouped = chunk_grouped()
         chunk_tiles(w_raw[1], range(TILES), w_grouped)
+        new_group()
         rotate(0, 4, accs[0])
         rotate(0, 5, accs[1])
         quantise_chunk(w_mx[1], w_grouped)
-        sum_pair_behind_quantise(0, 2, w_grouped)
-        pair(0, 3)
-        pair(1, 0)
+        sum_behind_quantise(w_grouped)
+        new_group()
+        token_tile(0, 6)
+        token_tile(0, 7)
+        sum_pair()
+        new_group()
+        token_tile(1, 0)
+        token_tile(1, 1)
         w_grouped = prepared(w_raw[2])
-        pair(1, 1)
+        sum_pair()
+        new_group()
+        token_tile(1, 2)
+        token_tile(1, 3)
         token_tile(1, 4)
         token_tile(1, 5)
         quantise_chunk(w_mx[2], w_grouped)
-        sum_pair_behind_quantise(1, 2, w_grouped)
+        sum_behind_quantise(w_grouped)
         v_grouped = prepared(v_raw)
-        pair(1, 3)
+        new_group()
+        token_tile(1, 6)
+        token_tile(1, 7)
         token_tile(2, 0)
         token_tile(2, 1)
         quantise_chunk(v_mx, v_grouped)
-        sum_pair_behind_quantise(2, 0, v_grouped)
+        sum_behind_quantise(v_grouped)
         w_grouped = prepared(w_raw[3])
-        pair(2, 1)
+        new_group()
+        token_tile(2, 2)
+        token_tile(2, 3)
         plain_tile(0)
         plain_tile(1)
         token_tile(2, 4)
         token_tile(2, 5)
+        accs = [project(2, 6), project(2, 7)]
+        w4_grouped = prepared(w_raw[4])
         quantise_chunk(w_mx[3], w_grouped)
-        sum_pair_behind_quantise(2, 2, w_grouped)
+        sum_behind_quantise(w_grouped)
+        new_group()
+        rotate(2, 6, accs[0])
+        rotate(2, 7, accs[1])
+        token_tile(3, 0)
+        token_tile(3, 1)
+        turn_tables()
         plain_tile(2)
         plain_tile(3)
-        turn_tables()
-        pair(2, 3)
-        pair(3, 0)
-        w_grouped = prepared(w_raw[4])
+        quantise_chunk(w_mx[4], w4_grouped)
+        sum_behind_quantise(w4_grouped)
         block = new_block(2)
         prods = [head_products(3, 0), head_products(3, 1)]
-        quantise_chunk(w_mx[4], w_grouped)
-        pair(3, 1)
+        new_group()
+        token_tile(3, 2)
+        token_tile(3, 3)
+        sum_pair()
+        plain_tile(4)
+        plain_tile(5)
+        new_group()
+        token_tile(4, 0)
+        token_tile(4, 1)
+        sum_pair()
         for h in (0, 1):
             head_sum(prods[h], block, h)
         store_block(block, 3, 0, 2)
-        plain_tile(4)
-        plain_tile(5)
-        pair(4, 0)
         plain_tile(6)
         plain_tile(7)
-        pair(4, 1)
-        pair(4, 2)
+        new_group()
+        token_tile(4, 2)
+        token_tile(4, 3)
+        sum_pair()
+        new_group()
+        token_tile(4, 4)
+        token_tile(4, 5)
+        sum_pair()
         prods = [head_products(3, 2), head_products(3, 3)]
-        for t in (6, 7):
-            token_tile(4, t)
+        new_group()
+        token_tile(4, 6)
+        token_tile(4, 7)
         block = new_block(2)
         for h in (0, 1):
             head_sum(prods[h], block, h)
         store_block(block, 3, 2, 4)
         rotated = rotated_pool.tile([P, 2 * HEADS, D], F32)
-        for t in (6, 7):
-            heads = slice((t % 2) * HEADS, (t % 2 + 1) * HEADS)
-            add(rotated[:, heads], pairs[4, 3][:, heads], nc.vector if t == 7 else nc.gpsimd)
-            store(rotated[:, heads], 4, t, t + 1)
+        prod, members = groups[-1]
+        for i, (n, t) in enumerate(members):
+            heads = slice(i * HEADS, (i + 1) * HEADS)
+            add(rotated[:, heads], prod[:, heads], nc.vector if t == TOKEN_TILES - 1 else nc.gpsimd)
+            store(rotated[:, heads], n, t, t + 1)

from contextlib import ExitStack

import concourse.mybir as mybir
from concourse.masks import make_identity

F32 = mybir.dt.float32
BF16 = mybir.dt.bfloat16
U32 = mybir.dt.uint32
U8 = mybir.dt.uint8
FP8X4 = mybir.dt.float8_e4m3fn_x4
MULT = mybir.AluOpType.mult
ADD = mybir.AluOpType.add

P = 128
K = 1024
K_PASS = 512
PASSES = K // K_PASS
WORDS = K // 2
TILES = 4
CHUNK = TILES * P
HALF_CHUNK = CHUNK // 2
TOKEN_TILES = 8
D = 128
HALF = D // 2
HEADS = CHUNK // D
GROUP = 4
Q_CHUNKS = 4
FIRST_TABLES = 2

FLOPS = 2 * 1024 * 1024 * 3072


def tile_attention_pa_kernel(tc, hidden_states, cos, sin, wq, wk, wv, out_0, out_1, out_2):
    nc = tc.nc
    with ExitStack() as ctx:
        ctx.enter_context(tc.manual_schedule())
        const = ctx.enter_context(tc.tile_pool(name="const", bufs=1))
        raw_pool = ctx.enter_context(tc.tile_pool(name="raw", bufs=5))
        mx_pool = ctx.enter_context(tc.tile_pool(name="mx", bufs=1))
        tile_grouped_pool = ctx.enter_context(tc.tile_pool(name="tile_grouped", bufs=4))
        head_prod_pool = ctx.enter_context(tc.tile_pool(name="head_prod", bufs=2))
        half_grouped_pool = ctx.enter_context(tc.tile_pool(name="half_grouped", bufs=2))
        block_pool = ctx.enter_context(tc.tile_pool(name="block", bufs=2))
        w_grouped_pool = ctx.enter_context(tc.tile_pool(name="w_grouped", bufs=3))
        prod_pool = ctx.enter_context(tc.tile_pool(name="prod", bufs=3))
        rotated_pool = ctx.enter_context(tc.tile_pool(name="rotated", bufs=4))
        plain_pool = ctx.enter_context(tc.tile_pool(name="plain", bufs=3))
        scalar_banks = ctx.enter_context(tc.psum_pool(name="scalar_banks", bufs=4))
        vector_banks = ctx.enter_context(tc.psum_pool(name="vector_banks", bufs=4))

        x_rows = hidden_states[0].rearrange("(p t) k -> p t k", t=TOKEN_TILES)
        q_out = out_0[0].rearrange("(p t) h d -> p t (h d)", t=TOKEN_TILES)
        k_out = out_1[0].rearrange("(p t) h d -> p t (h d)", t=TOKEN_TILES)
        v_out = out_2[0].rearrange("(p t) h d -> p t (h d)", t=TOKEN_TILES)

        def weight_rows(w, c):
            return w[c * CHUNK : (c + 1) * CHUNK, :].rearrange("(i r) k -> r i k", r=P)

        rotated_rows = [weight_rows(wq, c) for c in range(Q_CHUNKS)] + [weight_rows(wk, 0)]
        rotated_out = [q_out[:, :, c * CHUNK : (c + 1) * CHUNK] for c in range(Q_CHUNKS)] + [k_out]

        def load(rows):
            raw = raw_pool.tile([P, TILES, K], BF16, tag="raw")
            for i in range(TILES):
                nc.sync.dma_start(out=raw[:, i, :], in_=rows[:, i, :])
            return raw

        x_raw = [raw_pool.tile([P, TILES, K], BF16, name="x_raw%d" % h, tag="raw") for h in range(2)]

        def load_x(t):
            nc.sync.dma_start(out=x_raw[t // TILES][:, t % TILES, :], in_=x_rows[:, t, :])

        tables = const.tile([P, 2, TOKEN_TILES, D], BF16)

        def load_tables(first, last):
            for a, table in enumerate((cos, sin)):
                rows = table.rearrange("(p t) o d -> p t (o d)", t=TOKEN_TILES)
                nc.sync.dma_start(out=tables[:, a, first:last], in_=rows[:, first:last, :])

        load_x(0)
        w_raw = [load(rotated_rows[0])]
        load_tables(0, FIRST_TABLES)
        load_x(1)
        load_x(2)
        load_tables(FIRST_TABLES, TOKEN_TILES)
        for t in range(3, TOKEN_TILES):
            load_x(t)
        w_raw.append(load(rotated_rows[1]))
        w_raw.append(load(rotated_rows[2]))

        identity = const.tile([P, P], F32)
        make_identity(nc, identity[:])
        swap = const.tile([P, P], F32)
        nc.gpsimd.tensor_copy(out=swap[:, 0:HALF], in_=identity[:, HALF:D])
        nc.gpsimd.tensor_copy(out=swap[:, HALF:D], in_=identity[:, 0:HALF])
        identity_bf16 = const.tile([P, P], BF16)
        make_identity(nc, identity_bf16[:])

        def transpose_tile(rows, grouped):
            words = rows.bitcast(F32)
            bank = scalar_banks.tile([P, WORDS], F32, tag="bank")
            for g in range(PASSES):
                for u in range(2):
                    nc.tensor.transpose(
                        bank[:, (2 * g + u) * P : (2 * g + u + 1) * P],
                        words[:, 2 * g * P + u : 2 * (g + 1) * P : 2],
                        identity[:],
                    )
            nc.scalar.copy(out=grouped, in_=bank[:].rearrange("p (g u r) -> p g r u", g=PASSES, u=2))

        def mx_tiles(name):
            codes = mx_pool.tile([P, PASSES * CHUNK], U32, name=name + "_codes", align_bytes=64)
            scales = mx_pool.tile([P, PASSES * CHUNK], U8, name=name + "_scales", align_bytes=64)
            return codes, scales

        x_mx = [mx_tiles("x%d" % h) for h in range(2)]
        w_mx = [mx_tiles("w%d" % n) for n in range(len(rotated_rows))]
        v_mx = mx_tiles("v")

        def one_tile(raw, i):
            grouped = tile_grouped_pool.tile([P, PASSES * P * 4], BF16, align_bytes=64)
            transpose_tile(raw[:, i, :], grouped[:].bitcast(F32).rearrange("p (g r u) -> p g r u", g=PASSES, u=2))
            return grouped

        def token_columns(t, g):
            if t < TILES:
                first = (PASSES * t + g) * P
            else:
                half, i = divmod(t - TILES, TILES // 2)
                first = (half * PASSES + g) * HALF_CHUNK + i * P
            return slice(first, first + P)

        def quantise_token_tile(t, grouped):
            codes, scales = x_mx[0]
            columns = slice(PASSES * t * P, PASSES * (t + 1) * P)
            nc.vector.quantize_mx(out=codes[:, columns].bitcast(FP8X4), scales=scales[:, columns], in_=grouped[:])

        def quantise_weight_tile(operand, i, grouped):
            codes, scales = operand
            for g in range(PASSES):
                columns = slice(g * CHUNK + i * P, g * CHUNK + (i + 1) * P)
                nc.vector.quantize_mx(
                    out=codes[:, columns].bitcast(FP8X4),
                    scales=scales[:, columns],
                    in_=grouped[:, g * 4 * P : (g + 1) * 4 * P],
                )

        def half_grouped():
            grouped = half_grouped_pool.tile([P, PASSES * HALF_CHUNK * 2], F32, align_bytes=64)
            return grouped

        def half_tiles(half, grouped):
            view = grouped[:].rearrange("p (g c u) -> p g c u", g=PASSES, u=2)
            for i in range(TILES // 2):
                transpose_tile(x_raw[1][:, half * (TILES // 2) + i, :], view[:, :, i * P : (i + 1) * P, :])

        def quantise_half(half, grouped):
            codes, scales = x_mx[1]
            columns = slice(half * PASSES * HALF_CHUNK, (half + 1) * PASSES * HALF_CHUNK)
            nc.vector.quantize_mx(
                out=codes[:, columns].bitcast(FP8X4), scales=scales[:, columns], in_=grouped[:].bitcast(BF16)
            )

        def chunk_grouped():
            grouped = w_grouped_pool.tile([P, PASSES * CHUNK * 2], F32, align_bytes=64)
            return grouped

        def chunk_tiles(raw, tiles, grouped):
            view = grouped[:].rearrange("p (g c u) -> p g c u", g=PASSES, u=2)
            for i in tiles:
                transpose_tile(raw[:, i, :], view[:, :, i * P : (i + 1) * P, :])

        def quantise_chunk(operand, grouped):
            codes, scales = operand
            nc.vector.quantize_mx(out=codes[:].bitcast(FP8X4), scales=scales[:], in_=grouped[:].bitcast(BF16))

        def multiply(bank, stationary, columns_of, moving):
            for g in range(PASSES):
                columns = columns_of(g)
                rows = slice(g * CHUNK, (g + 1) * CHUNK)
                nc.tensor.matmul_mx(
                    out=bank[:],
                    lhsT=stationary[0][:, columns].bitcast(FP8X4),
                    lhsT_scale=stationary[1][:, columns],
                    rhs=moving[0][:, rows].bitcast(FP8X4),
                    rhs_scale=moving[1][:, rows],
                    start=(g == 0),
                    stop=(g == PASSES - 1),
                )

        def multiply_half(bank, stationary, h, half):
            for g in range(PASSES):
                columns = slice(g * CHUNK + h * P, g * CHUNK + (h + 1) * P)
                tokens = slice((half * PASSES + g) * HALF_CHUNK, (half * PASSES + g + 1) * HALF_CHUNK)
                nc.tensor.matmul_mx(
                    out=bank,
                    lhsT=stationary[0][:, columns].bitcast(FP8X4),
                    lhsT_scale=stationary[1][:, columns],
                    rhs=x_mx[1][0][:, tokens].bitcast(FP8X4),
                    rhs_scale=x_mx[1][1][:, tokens],
                    start=(g == 0),
                    stop=(g == PASSES - 1),
                )

        rot = const.tile([P, TOKEN_TILES, 2, 2, HALF], BF16)

        def build_rotation(first, last, copy, multiply_by):
            tokens = slice(first, last)
            copy(out=rot[:, tokens, 0, 0, :], in_=tables[:, 0, tokens, 0:HALF])
            copy(out=rot[:, tokens, 1, 1, :], in_=tables[:, 0, tokens, HALF:D])
            copy(out=rot[:, tokens, 0, 1, :], in_=tables[:, 1, tokens, HALF:D])
            multiply_by(rot[:, tokens, 1, 0, :], tables[:, 1, tokens, 0:HALF], -1.0)

        def project(n, t):
            acc = vector_banks.tile([P, CHUNK], F32, tag="acc")
            multiply(acc, x_mx[t // TILES], lambda g: token_columns(t, g), w_mx[n])
            return acc

        def products(prod, t, acc):
            nc.vector.tensor_tensor(
                out=prod.rearrange("p h s (o j) -> p h s o j", o=2),
                in0=acc[:]
                .rearrange("p (h s j) -> p h s j", s=2, j=HALF)
                .unsqueeze(3)
                .to_broadcast([P, HEADS, 2, 2, HALF]),
                in1=rot[:, t].unsqueeze(1).to_broadcast([P, HEADS, 2, 2, HALF]),
                op=MULT,
            )

        def add(rotated, prod, adder):
            adder.tensor_tensor(out=rotated, in0=prod[:, :, 0, :], in1=prod[:, :, 1, :], op=ADD)

        def store(rotated, n, first, last):
            nc.sync.dma_start(
                out=rotated_out[n][:, first:last, :],
                in_=rotated.rearrange("p (t h) d -> p t (h d)", h=HEADS),
            )

        turned = const.tile([P, 2, CHUNK], BF16)

        def turn_tables():
            flat = rot[:].rearrange("p t s o j -> p t (s o j)")
            for a in range(2):
                bank = scalar_banks.tile([P, CHUNK], BF16, tag="bank")
                for i in range(TILES):
                    t = TILES + i
                    table = flat[:, t, HALF : HALF + D] if a else tables[:, 0, t, :]
                    nc.tensor.transpose(bank[:, i * P : (i + 1) * P], table, identity_bf16[:])
                nc.scalar.copy(out=turned[:, a, :], in_=bank[:])

        def head_products(n, h):
            acc = vector_banks.tile([P, CHUNK], F32, tag="acc")
            for half in range(2):
                multiply_half(acc[:, half * HALF_CHUNK : (half + 1) * HALF_CHUNK], w_mx[n], h, half)
            prod = head_prod_pool.tile([P, 2, CHUNK], F32)
            nc.vector.tensor_tensor(
                out=prod[:], in0=acc[:].unsqueeze(1).to_broadcast([P, 2, CHUNK]), in1=turned[:], op=MULT
            )
            return prod

        def head_sum(prod, block, h):
            bank = scalar_banks.tile([P, TILES, D], F32, tag="bank")
            for i in range(TILES):
                for a, order in enumerate((identity, swap)):
                    nc.tensor.matmul(
                        bank[:, i, :],
                        lhsT=prod[:, a, i * P : (i + 1) * P],
                        rhs=order[:],
                        is_transpose=True,
                        start=(a == 0),
                        stop=(a == 1),
                    )
            nc.scalar.copy(out=block[:, :, h * D : (h + 1) * D], in_=bank[:])

        def new_block(heads):
            block = block_pool.tile([P, TILES, heads * D], F32)
            return block

        def store_block(block, n, first, last):
            nc.sync.dma_start(out=rotated_out[n][:, TILES:TOKEN_TILES, first * D : last * D], in_=block[:])

        plain_tiles = []

        def plain_tile(t):
            if t % 2 == 0:
                plain = plain_pool.tile([P, 2, CHUNK], F32)
                plain_tiles.append(plain)
            plain = plain_tiles[-1]
            bank = scalar_banks.tile([P, CHUNK], F32, tag="bank")
            multiply(bank, x_mx[t // TILES], lambda g: token_columns(t, g), v_mx)
            nc.scalar.copy(out=plain[:, t % 2, :], in_=bank[:])
            if t % 2 == 1:
                nc.sync.dma_start(out=v_out[:, t - 1 : t + 1, :], in_=plain[:])

        groups = []

        def new_group():
            prod = prod_pool.tile([P, GROUP * HEADS, 2, D], F32)
            groups.append((prod, []))

        def rotate(n, t, acc):
            prod, members = groups[-1]
            first = len(members) * HEADS
            products(prod[:, first : first + HEADS], t, acc)
            members.append((n, t))

        def token_tile(n, t):
            rotate(n, t, project(n, t))

        def sum_group(rotated):
            prod, members = groups[-1]
            add(rotated, prod[:, 0 : len(members) * HEADS], nc.gpsimd)
            for i in range(0, len(members), 2):
                n, t = members[i]
                store(rotated[:, i * HEADS : (i + 2) * HEADS], n, t, t + 2)

        def sum_behind_quantise(grouped):
            width = len(groups[-1][1]) * HEADS * D
            sum_group(grouped[:, 0:width].rearrange("p (h d) -> p h d", d=D))

        def sum_pair():
            rotated = rotated_pool.tile([P, 2 * HEADS, D], F32)
            sum_group(rotated[:])

        def prepared(raw):
            grouped = chunk_grouped()
            chunk_tiles(raw, range(TILES), grouped)
            return grouped

        grouped = one_tile(x_raw[0], 0)
        quantise_token_tile(0, grouped)
        for i in range(TILES):
            grouped = one_tile(w_raw[0], i)
            quantise_weight_tile(w_mx[0], i, grouped)
        build_rotation(0, FIRST_TABLES, nc.vector.tensor_copy, nc.vector.tensor_scalar_mul)
        grouped = one_tile(x_raw[0], 1)
        quantise_token_tile(1, grouped)
        grouped2 = one_tile(x_raw[0], 2)
        build_rotation(FIRST_TABLES, TOKEN_TILES, nc.scalar.copy, nc.scalar.mul)

        accs = [project(0, 0), project(0, 1)]
        new_group()
        rotate(0, 0, accs[0])
        quantise_token_tile(2, grouped2)
        grouped3 = one_tile(x_raw[0], 3)
        v_raw = load(weight_rows(wv, 0))
        rotate(0, 1, accs[1])
        quantise_token_tile(3, grouped3)
        x_halves = [half_grouped(), half_grouped()]
        half_tiles(0, x_halves[0])
        accs = [project(0, 2), project(0, 3)]
        half_tiles(1, x_halves[1])
        w_raw.append(load(rotated_rows[3]))
        w_raw.append(load(rotated_rows[4]))
        quantise_half(0, x_halves[0])
        sum_behind_quantise(x_halves[0])
        new_group()
        rotate(0, 2, accs[0])
        rotate(0, 3, accs[1])
        accs = [project(0, 4), project(0, 5)]
        quantise_half(1, x_halves[1])
        sum_behind_quantise(x_halves[1])
        w_grouped = chunk_grouped()
        chunk_tiles(w_raw[1], range(TILES), w_grouped)
        new_group()
        rotate(0, 4, accs[0])
        rotate(0, 5, accs[1])
        quantise_chunk(w_mx[1], w_grouped)
        sum_behind_quantise(w_grouped)
        new_group()
        token_tile(0, 6)
        token_tile(0, 7)
        sum_pair()
        new_group()
        token_tile(1, 0)
        token_tile(1, 1)
        w_grouped = prepared(w_raw[2])
        sum_pair()
        new_group()
        token_tile(1, 2)
        token_tile(1, 3)
        token_tile(1, 4)
        token_tile(1, 5)
        quantise_chunk(w_mx[2], w_grouped)
        sum_behind_quantise(w_grouped)
        v_grouped = prepared(v_raw)
        new_group()
        token_tile(1, 6)
        token_tile(1, 7)
        token_tile(2, 0)
        token_tile(2, 1)
        quantise_chunk(v_mx, v_grouped)
        sum_behind_quantise(v_grouped)
        w_grouped = prepared(w_raw[3])
        new_group()
        token_tile(2, 2)
        token_tile(2, 3)
        plain_tile(0)
        plain_tile(1)
        token_tile(2, 4)
        token_tile(2, 5)
        accs = [project(2, 6), project(2, 7)]
        w4_grouped = prepared(w_raw[4])
        quantise_chunk(w_mx[3], w_grouped)
        sum_behind_quantise(w_grouped)
        new_group()
        rotate(2, 6, accs[0])
        rotate(2, 7, accs[1])
        token_tile(3, 0)
        token_tile(3, 1)
        turn_tables()
        plain_tile(2)
        plain_tile(3)
        quantise_chunk(w_mx[4], w4_grouped)
        sum_behind_quantise(w4_grouped)
        block = new_block(2)
        prods = [head_products(3, 0), head_products(3, 1)]
        new_group()
        token_tile(3, 2)
        token_tile(3, 3)
        sum_pair()
        plain_tile(4)
        plain_tile(5)
        new_group()
        token_tile(4, 0)
        token_tile(4, 1)
        sum_pair()
        for h in (0, 1):
            head_sum(prods[h], block, h)
        store_block(block, 3, 0, 2)
        plain_tile(6)
        plain_tile(7)
        new_group()
        token_tile(4, 2)
        token_tile(4, 3)
        sum_pair()
        new_group()
        token_tile(4, 4)
        token_tile(4, 5)
        sum_pair()
        prods = [head_products(3, 2), head_products(3, 3)]
        new_group()
        token_tile(4, 6)
        token_tile(4, 7)
        block = new_block(2)
        for h in (0, 1):
            head_sum(prods[h], block, h)
        store_block(block, 3, 2, 4)
        rotated = rotated_pool.tile([P, 2 * HEADS, D], F32)
        prod, members = groups[-1]
        for i, (n, t) in enumerate(members):
            heads = slice(i * HEADS, (i + 1) * HEADS)
            add(rotated[:, heads], prod[:, heads], nc.vector if t == TOKEN_TILES - 1 else nc.gpsimd)
            store(rotated[:, heads], n, t, t + 1)
